import numpy as np
import ml_dtypes


def mxq(x, axis, fmt="e4m3"):
    dtype, down = {"e4m3": (ml_dtypes.float8_e4m3fn, 7), "e5m2": (ml_dtypes.float8_e5m2, 14)}[fmt]
    v = np.moveaxis(np.asarray(x, np.float32).astype(ml_dtypes.bfloat16).astype(np.float64), axis, -1)
    blocks = v.reshape(v.shape[:-1] + (-1, 32))
    amax = np.abs(blocks).max(-1, keepdims=True)
    byte = np.maximum(np.where(amax > 0, np.frexp(amax)[1] - 1 + 127, 0) - down, 1)
    scale = np.exp2(byte - 127.0)
    codes = (blocks / scale).astype(np.float32).astype(dtype).astype(np.float64)
    return np.moveaxis((codes * scale).reshape(v.shape), -1, axis)


WIDE = False


def mx_kscale(k):
    if not WIDE:
        return np.ones(k)
    levels = np.array([10, -10, 5, -5, 0])
    a = np.random.permutation(np.resize(levels, k // 512 * 4)).reshape(k // 512, 4)
    idx = np.arange(k)
    return np.exp2(a[idx // 512, idx % 128 // 32])


BF16 = ml_dtypes.bfloat16


def bf(x):
    return np.asarray(x, np.float32).astype(BF16)


def f64(x):
    return np.asarray(x).astype(np.float64)


E2M1 = np.array([0.0, 0.5, 1.0, 1.5, 2.0, 3.0, 4.0, 6.0, -0.0, -0.5, -1.0, -1.5, -2.0, -3.0, -4.0, -6.0])


def pack_weight(w, fmt):
    k, n = w.shape
    w = f64(bf(w)).reshape(k // 32, 32, n)
    amax = np.abs(w).max(1)
    if fmt == "e4m3":
        byte = np.frexp(amax)[1] - 1 + 127 - 7
    else:
        mant, ex = np.frexp(amax / 6.0)
        byte = np.where(mant > 0.5, ex, ex - 1) + 127
    byte = np.clip(np.where(amax > 0, byte, 1), 1, 254)
    scaled = (w * np.exp2(127.0 - byte)[:, None, :]).reshape(k, n).astype(np.float32)
    by_word = np.ascontiguousarray(scaled.reshape(k // 512, 128, 4, n).transpose(0, 1, 3, 2))
    if fmt == "e4m3":
        words = by_word.astype(ml_dtypes.float8_e4m3fn).view(np.uint8)
    else:
        c = by_word.astype(ml_dtypes.float4_e2m1fn).view(np.uint8) & 0xF
        words = c[..., 0::2] | (c[..., 1::2] << 4)
    return np.ascontiguousarray(words), np.ascontiguousarray(byte.astype(np.uint8).reshape(k // 512, 16, n))


def unpack_weight(words, scales, fmt):
    g, p, n, _ = words.shape
    if fmt == "e4m3":
        vals = np.ascontiguousarray(words).view(ml_dtypes.float8_e4m3fn).astype(np.float64)
    else:
        nib = np.empty((g, p, n, 4), np.uint8)
        nib[..., 0::2] = words & 0xF
        nib[..., 1::2] = words >> 4
        vals = E2M1[nib]
    vals = vals * np.repeat(np.exp2(scales.astype(np.float64) - 127.0), 8, axis=1)[..., None]
    return vals.transpose(0, 1, 3, 2).reshape(g * 512, n)


BATCH, SEQ, IN_DIM, MID_DIM, OUT_DIM = 4, 128, 2048, 2048, 2048
CB = 2.0 ** -np.round(np.log2(IN_DIM) / 2)
CA = 2.0 ** -np.round(np.log2(MID_DIM) / 2)
FMT = "e4m3"


def signs(shape):
    return np.where(np.random.standard_normal(shape) >= 0, 1.0, -1.0)


def setup_inputs():
    s, t = mx_kscale(IN_DIM), mx_kscale(MID_DIM)
    x = bf(np.random.standard_normal((BATCH, SEQ, IN_DIM)) * s)
    scaling0 = bf(0.5 + np.random.uniform(size=IN_DIM))
    B_words, B_scales = pack_weight((signs((MID_DIM, IN_DIM)) * CB / s[None, :]).T, FMT)
    scaling2 = bf((0.5 + np.random.uniform(size=MID_DIM)) * t)
    A_words, A_scales = pack_weight((signs((OUT_DIM, MID_DIM)) * CA / t[None, :]).T, FMT)
    scaling4 = bf(0.5 + np.random.uniform(size=OUT_DIM))
    bias = bf(np.random.standard_normal(OUT_DIM))
    return {"x": x,
            "scaling0": scaling0,
            "B_words": B_words,
            "B_scales": B_scales,
            "scaling2": scaling2,
            "A_words": A_words,
            "A_scales": A_scales,
            "scaling4": scaling4,
            "bias": bias}


def reference(x, scaling0, B_words, B_scales, scaling2, A_words, A_scales, scaling4, bias):
    h = f64(x) * f64(scaling0)
    h = mxq(h, 2, "e4m3") @ unpack_weight(B_words, B_scales, FMT)
    h = h * f64(scaling2)
    h = mxq(h, 2, "e4m3") @ unpack_weight(A_words, A_scales, FMT)
    return h * f64(scaling4) + f64(bias)

@@ -1,0 +1,168 @@
+import concourse.mybir as mybir
+from concourse.masks import make_identity
+
+F32 = mybir.dt.float32
+BF16 = mybir.dt.bfloat16
+I32 = mybir.dt.int32
+U32 = mybir.dt.uint32
+U8 = mybir.dt.uint8
+FP8X4 = mybir.dt.float8_e4m3fn_x4
+MULT = mybir.AluOpType.mult
+ADD = mybir.AluOpType.add
+
+P = 128
+PACK = 4
+K_PASS = P * PACK
+TOKENS = 512
+DIM = 2048
+TOKEN_TILES = TOKENS // P
+PASSES = DIM // K_PASS
+N_TILE = 512
+CHUNKS = DIM // N_TILE
+QUADRANTS = 4
+WORDS_PER_PASS = K_PASS // 2
+
+FLOPS = 2 * 2 * TOKENS * DIM * DIM
+
+
+def load_scale_planes(nc, planes, scales):
+    for quadrant in range(QUADRANTS):
+        nc.sync.dma_start(
+            out=planes[32 * quadrant : 32 * quadrant + 4 * PASSES, :].bitcast(I32),
+            in_=scales[:, 4 * quadrant : 4 * quadrant + 4, :].bitcast(I32),
+        )
+
+
+def load_word_chunk(nc, words, words_dram, chunk):
+    byte_cols = slice(chunk * N_TILE * PACK, (chunk + 1) * N_TILE * PACK)
+    nc.sync.dma_start(
+        out=words[:, :, chunk * N_TILE : (chunk + 1) * N_TILE].bitcast(I32),
+        in_=words_dram.rearrange("g p n t -> p g (n t)")[:, :, byte_cols].bitcast(I32),
+    )
+
+
+def mx_output_tile(nc, acc, act_words, act_scales, weight_words, weight_planes, cols):
+    for g in range(PASSES):
+        nc.tensor.matmul_mx(
+            out=acc,
+            lhsT=act_words[:, g, :].bitcast(FP8X4),
+            lhsT_scale=act_scales[:, g, :],
+            rhs=weight_words[:, g, cols].bitcast(FP8X4),
+            rhs_scale=weight_planes[4 * g : P, cols],
+            start=(g == 0),
+            stop=(g == PASSES - 1),
+        )
+
+
+def tile_doublebinarylinear_kernel(
+    tc, x, scaling0, B_words, B_scales, scaling2, A_words, A_scales, scaling4, bias, out
+):
+    nc = tc.nc
+    x_rows = x.flatten_outer_dims()
+    out_rows = out.flatten_outer_dims()
+
+    with tc.tile_pool(name="keep", bufs=1) as keep, tc.tile_pool(name="work", bufs=2) as work, tc.psum_pool(
+        name="psum", bufs=1
+    ) as psum, tc.manual_schedule():
+        x_sb = keep.tile([P, TOKEN_TILES, DIM], BF16)
+        s0_by_k = keep.tile([P, PASSES, PACK], BF16)
+        s2_all = keep.tile([P, DIM], BF16)
+        s4_all = keep.tile([P, DIM], BF16)
+        bias_all = keep.tile([P, DIM], BF16)
+        b_words = keep.tile([P, PASSES, DIM], U32, align_bytes=64)
+        a_words = keep.tile([P, PASSES, DIM], U32, align_bytes=64)
+        b_planes = keep.tile([P, DIM], U8, align_bytes=64)
+        a_planes = keep.tile([P, DIM], U8, align_bytes=64)
+        h0_words = keep.tile([P, TOKEN_TILES, PASSES, P], U32, align_bytes=64)
+        h0_scales = keep.tile([P, TOKEN_TILES, PASSES, P], U8, align_bytes=64)
+        h2_words = keep.tile([P, PASSES, TOKENS], U32, align_bytes=64)
+        h2_scales = keep.tile([P, PASSES, TOKENS], U8, align_bytes=64)
+        ident_f32 = keep.tile([P, P], F32)
+        ident_bf16 = keep.tile([P, P], BF16)
+
+        nc.vector.memset(b_planes[:].bitcast(I32), 0)
+        nc.vector.memset(a_planes[:].bitcast(I32), 0)
+        make_identity(nc, ident_f32[:])
+        make_identity(nc, ident_bf16[:])
+
+        nc.sync.dma_start(out=s0_by_k[:], in_=scaling0.rearrange("(g p t) -> p g t", g=PASSES, p=P))
+        for i in range(TOKEN_TILES):
+            nc.sync.dma_start(out=x_sb[:, i, :], in_=x_rows[i * P : (i + 1) * P, :])
+        load_scale_planes(nc, b_planes, B_scales)
+        load_word_chunk(nc, b_words, B_words, 0)
+        nc.sync.dma_start(out=s2_all[:], in_=scaling2.partition_broadcast(P))
+        for c in range(1, CHUNKS):
+            load_word_chunk(nc, b_words, B_words, c)
+        load_scale_planes(nc, a_planes, A_scales)
+        load_word_chunk(nc, a_words, A_words, 0)
+        nc.sync.dma_start(out=s4_all[:], in_=scaling4.partition_broadcast(P))
+        nc.sync.dma_start(out=bias_all[:], in_=bias.partition_broadcast(P))
+        for c in range(1, CHUNKS):
+            load_word_chunk(nc, a_words, A_words, c)
+
+        for i in range(TOKEN_TILES):
+            x_pairs = x_sb[:, i, :].bitcast(F32)
+            x_by_k = work.tile([P, PASSES, P, PACK], BF16)
+            for half in range(PASSES // 2):
+                pairs_t = psum.tile([P, 2, 2, P], F32, tag="transposed", bufs=3)
+                for gg in range(2):
+                    first = (2 * half + gg) * WORDS_PER_PASS
+                    for u in range(2):
+                        nc.tensor.transpose(
+                            pairs_t[:, gg, u, :], x_pairs[:, first + u : first + WORDS_PER_PASS : 2], ident_f32[:]
+                        )
+                nc.scalar.copy(
+                    out=x_by_k[:, 2 * half : 2 * half + 2].bitcast(F32),
+                    in_=pairs_t[:].rearrange("p g u r -> p g r u"),
+                )
+            h0 = work.tile([P, PASSES, P, PACK], BF16, align_bytes=64)
+            nc.vector.tensor_tensor(
+                out=h0[:],
+                in0=x_by_k[:],
+                in1=s0_by_k[:].unsqueeze(2).to_broadcast([P, PASSES, P, PACK]),
+                op=MULT,
+            )
+            nc.vector.quantize_mx(
+                out=h0_words[:, i].rearrange("p g r -> p (g r)").bitcast(FP8X4),
+                scales=h0_scales[:, i].rearrange("p g r -> p (g r)"),
+                in_=h0[:].rearrange("p g r t -> p (g r t)"),
+            )
+
+        for c in range(CHUNKS):
+            cols = slice(c * N_TILE, (c + 1) * N_TILE)
+            h2_of_tile = []
+            for i in range(TOKEN_TILES):
+                acc = psum.tile([P, N_TILE], F32, tag="acc", bufs=5)
+                mx_output_tile(nc, acc[:], h0_words[:, i], h0_scales[:, i], b_words, b_planes, cols)
+                h2 = work.tile([P, PACK, P], BF16, bufs=6)
+                nc.vector.tensor_tensor(
+                    out=h2[:],
+                    in0=acc[:].rearrange("r (p t) -> r t p", t=PACK),
+                    in1=s2_all[:, cols].rearrange("r (p t) -> r t p", t=PACK),
+                    op=MULT,
+                )
+                h2_of_tile.append(h2)
+            for i in range(TOKEN_TILES):
+                rows = slice(i * P, (i + 1) * P)
+                h2_t = psum.tile([P, PACK, P], BF16, tag="transposed", bufs=3)
+                for t in range(PACK):
+                    nc.tensor.transpose(h2_t[:, t, :], h2_of_tile[i][:, t, :], ident_bf16[:])
+                h2_by_k = work.tile([P, P, PACK], BF16, bufs=3, align_bytes=64)
+                nc.scalar.copy(out=h2_by_k[:], in_=h2_t[:].rearrange("p t r -> p r t"))
+                nc.vector.quantize_mx(
+                    out=h2_words[:, c, rows].bitcast(FP8X4),
+                    scales=h2_scales[:, c, rows],
+                    in_=h2_by_k[:].rearrange("p r t -> p (r t)"),
+                )
+
+        for c in range(CHUNKS):
+            cols = slice(c * N_TILE, (c + 1) * N_TILE)
+            for i in range(TOKEN_TILES):
+                rows = slice(i * P, (i + 1) * P)
+                acc = psum.tile([P, N_TILE], F32, tag="acc", bufs=5)
+                mx_output_tile(nc, acc[:], h2_words[:, :, rows], h2_scales[:, :, rows], a_words, a_planes, cols)
+                result = work.tile([P, N_TILE], F32, bufs=4)
+                nc.vector.tensor_tensor(out=result[:], in0=acc[:], in1=s4_all[:, cols], op=MULT)
+                adder = nc.gpsimd if i % 2 == 0 else nc.vector
+                adder.tensor_tensor(out=result[:], in0=result[:], in1=bias_all[:, cols], op=ADD)
+                nc.sync.dma_start(out=out_rows[rows, cols], in_=result[:])

@@ -78,12 +78,10 @@ def tile_doublebinarylinear_kernel(
         h2_words = keep.tile([P, PASSES, TOKENS], U32, align_bytes=64)
         h2_scales = keep.tile([P, PASSES, TOKENS], U8, align_bytes=64)
         ident_f32 = keep.tile([P, P], F32)
-        ident_bf16 = keep.tile([P, P], BF16)
 
         nc.vector.memset(b_planes[:].bitcast(I32), 0)
         nc.vector.memset(a_planes[:].bitcast(I32), 0)
         make_identity(nc, ident_f32[:])
-        make_identity(nc, ident_bf16[:])
 
         nc.sync.dma_start(out=s0_by_k[:], in_=scaling0.rearrange("(g p t) -> p g t", g=PASSES, p=P))
         for i in range(TOKEN_TILES):
@@ -134,25 +132,27 @@ def tile_doublebinarylinear_kernel(
             for i in range(TOKEN_TILES):
                 acc = psum.tile([P, N_TILE], F32, tag="acc", bufs=5)
                 mx_output_tile(nc, acc[:], h0_words[:, i], h0_scales[:, i], b_words, b_planes, cols)
-                h2 = work.tile([P, PACK, P], BF16, bufs=6)
+                h2 = work.tile([P, 2, P, 2], BF16, bufs=6)
                 nc.vector.tensor_tensor(
                     out=h2[:],
-                    in0=acc[:].rearrange("r (p t) -> r t p", t=PACK),
-                    in1=s2_all[:, cols].rearrange("r (p t) -> r t p", t=PACK),
+                    in0=acc[:].rearrange("r (p u e) -> r u p e", u=2, e=2),
+                    in1=s2_all[:, cols].rearrange("r (p u e) -> r u p e", u=2, e=2),
                     op=MULT,
                 )
                 h2_of_tile.append(h2)
-            for i in range(TOKEN_TILES):
-                rows = slice(i * P, (i + 1) * P)
-                h2_t = psum.tile([P, PACK, P], BF16, tag="transposed", bufs=3)
-                for t in range(PACK):
-                    nc.tensor.transpose(h2_t[:, t, :], h2_of_tile[i][:, t, :], ident_bf16[:])
-                h2_by_k = work.tile([P, P, PACK], BF16, bufs=3, align_bytes=64)
-                nc.scalar.copy(out=h2_by_k[:], in_=h2_t[:].rearrange("p t r -> p r t"))
+            for pair in range(TOKEN_TILES // 2):
+                rows = slice(pair * 2 * P, (pair + 1) * 2 * P)
+                h2_t = psum.tile([P, 2, 2, P], F32, tag="transposed", bufs=3)
+                for j in range(2):
+                    for u in range(2):
+                        h2_words_u = h2_of_tile[2 * pair + j][:, u].rearrange("r p e -> r (p e)").bitcast(F32)
+                        nc.tensor.transpose(h2_t[:, j, u, :], h2_words_u, ident_f32[:])
+                h2_by_k = work.tile([P, 2, P, PACK], BF16, bufs=3, align_bytes=64)
+                nc.scalar.copy(out=h2_by_k[:].bitcast(F32), in_=h2_t[:].rearrange("p j u r -> p j r u"))
                 nc.vector.quantize_mx(
                     out=h2_words[:, c, rows].bitcast(FP8X4),
                     scales=h2_scales[:, c, rows],
-                    in_=h2_by_k[:].rearrange("p r t -> p (r t)"),
+                    in_=h2_by_k[:].rearrange("p j r t -> p (j r t)"),
                 )
 
         for c in range(CHUNKS):

@@ -83,12 +83,17 @@ def tile_doublebinarylinear_kernel(
         nc.vector.memset(a_planes[:].bitcast(I32), 0)
         make_identity(nc, ident_f32[:])
 
-        nc.sync.dma_start(out=s0_by_k[:], in_=scaling0.rearrange("(g p t) -> p g t", g=PASSES, p=P))
-        for i in range(TOKEN_TILES):
+        def load_x(i):
             nc.sync.dma_start(out=x_sb[:, i, :], in_=x_rows[i * P : (i + 1) * P, :])
+
+        nc.sync.dma_start(out=s0_by_k[:], in_=scaling0.rearrange("(g p t) -> p g t", g=PASSES, p=P))
+        load_x(0)
+        load_x(1)
         load_scale_planes(nc, b_planes, B_scales)
         load_word_chunk(nc, b_words, B_words, 0)
+        load_x(2)
         nc.sync.dma_start(out=s2_all[:], in_=scaling2.partition_broadcast(P))
+        load_x(3)
         for c in range(1, CHUNKS):
             load_word_chunk(nc, b_words, B_words, c)
         load_scale_planes(nc, a_planes, A_scales)
@@ -98,9 +103,9 @@ def tile_doublebinarylinear_kernel(
         for c in range(1, CHUNKS):
             load_word_chunk(nc, a_words, A_words, c)
 
-        for i in range(TOKEN_TILES):
+        def quantise_x(i):
             x_pairs = x_sb[:, i, :].bitcast(F32)
-            x_by_k = work.tile([P, PASSES, P, PACK], BF16)
+            h0 = work.tile([P, PASSES, P, PACK], BF16, align_bytes=64)
             for half in range(PASSES // 2):
                 pairs_t = psum.tile([P, 2, 2, P], F32, tag="transposed", bufs=3)
                 for gg in range(2):
@@ -109,60 +114,82 @@ def tile_doublebinarylinear_kernel(
                         nc.tensor.transpose(
                             pairs_t[:, gg, u, :], x_pairs[:, first + u : first + WORDS_PER_PASS : 2], ident_f32[:]
                         )
-                nc.scalar.copy(
-                    out=x_by_k[:, 2 * half : 2 * half + 2].bitcast(F32),
-                    in_=pairs_t[:].rearrange("p g u r -> p g r u"),
-                )
-            h0 = work.tile([P, PASSES, P, PACK], BF16, align_bytes=64)
-            nc.vector.tensor_tensor(
-                out=h0[:],
-                in0=x_by_k[:],
-                in1=s0_by_k[:].unsqueeze(2).to_broadcast([P, PASSES, P, PACK]),
-                op=MULT,
-            )
+                for gg in range(2):
+                    g = 2 * half + gg
+                    x_t = pairs_t[:, gg].rearrange("p u r -> p (u r)").bitcast(BF16)
+                    nc.vector.tensor_tensor(
+                        out=h0[:, g].rearrange("p r (u e) -> p r u e", u=2),
+                        in0=x_t.rearrange("p (u r e) -> p r u e", u=2, e=2),
+                        in1=s0_by_k[:, g].rearrange("p (u e) -> p u e", u=2).unsqueeze(1).to_broadcast([P, P, 2, 2]),
+                        op=MULT,
+                    )
             nc.vector.quantize_mx(
                 out=h0_words[:, i].rearrange("p g r -> p (g r)").bitcast(FP8X4),
                 scales=h0_scales[:, i].rearrange("p g r -> p (g r)"),
                 in_=h0[:].rearrange("p g r t -> p (g r t)"),
             )
 
-        for c in range(CHUNKS):
-            cols = slice(c * N_TILE, (c + 1) * N_TILE)
-            h2_of_tile = []
-            for i in range(TOKEN_TILES):
-                acc = psum.tile([P, N_TILE], F32, tag="acc", bufs=5)
-                mx_output_tile(nc, acc[:], h0_words[:, i], h0_scales[:, i], b_words, b_planes, cols)
-                h2 = work.tile([P, 2, P, 2], BF16, bufs=6)
-                nc.vector.tensor_tensor(
-                    out=h2[:],
-                    in0=acc[:].rearrange("r (p u e) -> r u p e", u=2, e=2),
-                    in1=s2_all[:, cols].rearrange("r (p u e) -> r u p e", u=2, e=2),
-                    op=MULT,
-                )
-                h2_of_tile.append(h2)
-            for pair in range(TOKEN_TILES // 2):
-                rows = slice(pair * 2 * P, (pair + 1) * 2 * P)
-                h2_t = psum.tile([P, 2, 2, P], F32, tag="transposed", bufs=3)
-                for j in range(2):
-                    for u in range(2):
-                        h2_words_u = h2_of_tile[2 * pair + j][:, u].rearrange("r p e -> r (p e)").bitcast(F32)
-                        nc.tensor.transpose(h2_t[:, j, u, :], h2_words_u, ident_f32[:])
-                h2_by_k = work.tile([P, 2, P, PACK], BF16, bufs=3, align_bytes=64)
-                nc.scalar.copy(out=h2_by_k[:].bitcast(F32), in_=h2_t[:].rearrange("p j u r -> p j r u"))
-                nc.vector.quantize_mx(
-                    out=h2_words[:, c, rows].bitcast(FP8X4),
-                    scales=h2_scales[:, c, rows],
-                    in_=h2_by_k[:].rearrange("p j r t -> p (j r t)"),
-                )
+        h2_tiles = {}
 
-        for c in range(CHUNKS):
+        def first_product(i, c):
             cols = slice(c * N_TILE, (c + 1) * N_TILE)
+            acc = psum.tile([P, N_TILE], F32, tag="acc", bufs=5)
+            mx_output_tile(nc, acc[:], h0_words[:, i], h0_scales[:, i], b_words, b_planes, cols)
+            h2 = work.tile([P, 2, P, 2], BF16, bufs=8)
+            nc.vector.tensor_tensor(
+                out=h2[:],
+                in0=acc[:].rearrange("r (p u e) -> r u p e", u=2, e=2),
+                in1=s2_all[:, cols].rearrange("r (p u e) -> r u p e", u=2, e=2),
+                op=MULT,
+            )
+            h2_tiles[i, c] = h2
+
+        def quantise_h2(pair, c):
+            rows = slice(pair * 2 * P, (pair + 1) * 2 * P)
+            h2_t = psum.tile([P, 2, 2, P], F32, tag="transposed", bufs=3)
+            for j in range(2):
+                for u in range(2):
+                    h2_words_u = h2_tiles[2 * pair + j, c][:, u].rearrange("r p e -> r (p e)").bitcast(F32)
+                    nc.tensor.transpose(h2_t[:, j, u, :], h2_words_u, ident_f32[:])
+            h2_by_k = work.tile([P, 2, P, PACK], BF16, bufs=3, align_bytes=64)
+            nc.scalar.copy(out=h2_by_k[:].bitcast(F32), in_=h2_t[:].rearrange("p j u r -> p j r u"))
+            nc.vector.quantize_mx(
+                out=h2_words[:, c, rows].bitcast(FP8X4),
+                scales=h2_scales[:, c, rows],
+                in_=h2_by_k[:].rearrange("p j r t -> p (j r t)"),
+            )
+
+        def second_product(i, c):
+            rows = slice(i * P, (i + 1) * P)
+            cols = slice(c * N_TILE, (c + 1) * N_TILE)
+            acc = psum.tile([P, N_TILE], F32, tag="acc", bufs=5)
+            mx_output_tile(nc, acc[:], h2_words[:, :, rows], h2_scales[:, :, rows], a_words, a_planes, cols)
+            result = work.tile([P, N_TILE], F32, bufs=4)
+            nc.vector.tensor_tensor(out=result[:], in0=acc[:], in1=s4_all[:, cols], op=MULT)
+            adder = nc.gpsimd if i % 2 == 0 else nc.vector
+            adder.tensor_tensor(out=result[:], in0=result[:], in1=bias_all[:, cols], op=ADD)
+            nc.sync.dma_start(out=out_rows[rows, cols], in_=result[:])
+
+        quantise_x(0)
+        quantise_x(1)
+        first_product(0, 0)
+        quantise_x(2)
+        quantise_x(3)
+        for i in range(1, TOKEN_TILES):
+            first_product(i, 0)
+        for c in range(1, CHUNKS):
+            first_product(0, c)
+            first_product(1, c)
+            quantise_h2(0, c - 1)
+            quantise_h2(1, c - 1)
+            first_product(2, c)
+            if c == CHUNKS - 1:
+                quantise_h2(0, c)
+            first_product(3, c)
+        second_product(0, 0)
+        quantise_h2(1, CHUNKS - 1)
+        for i in range(1, TOKEN_TILES):
+            second_product(i, 0)
+        for c in range(1, CHUNKS):
             for i in range(TOKEN_TILES):
-                rows = slice(i * P, (i + 1) * P)
-                acc = psum.tile([P, N_TILE], F32, tag="acc", bufs=5)
-                mx_output_tile(nc, acc[:], h2_words[:, :, rows], h2_scales[:, :, rows], a_words, a_planes, cols)
-                result = work.tile([P, N_TILE], F32, bufs=4)
-                nc.vector.tensor_tensor(out=result[:], in0=acc[:], in1=s4_all[:, cols], op=MULT)
-                adder = nc.gpsimd if i % 2 == 0 else nc.vector
-                adder.tensor_tensor(out=result[:], in0=result[:], in1=bias_all[:, cols], op=ADD)
-                nc.sync.dma_start(out=out_rows[rows, cols], in_=result[:])
+                second_product(i, c)

@@ -78,7 +78,11 @@ def tile_doublebinarylinear_kernel(
         h2_words = keep.tile([P, PASSES, TOKENS], U32, align_bytes=64)
         h2_scales = keep.tile([P, PASSES, TOKENS], U8, align_bytes=64)
         ident_f32 = keep.tile([P, P], F32)
+        ones = keep.tile([P, P], BF16)
+        s2_row = keep.tile([P, DIM], BF16)
 
+        nc.vector.memset(s2_row[:].bitcast(I32), 0)
+        nc.vector.memset(ones[:], 1.0)
         nc.vector.memset(b_planes[:].bitcast(I32), 0)
         nc.vector.memset(a_planes[:].bitcast(I32), 0)
         make_identity(nc, ident_f32[:])
@@ -88,11 +92,11 @@ def tile_doublebinarylinear_kernel(
 
         nc.sync.dma_start(out=s0_by_k[:], in_=scaling0.rearrange("(g p t) -> p g t", g=PASSES, p=P))
         load_x(0)
+        nc.sync.dma_start(out=s2_row[0:1, :], in_=scaling2.rearrange("(o n) -> o n", o=1))
         load_x(1)
         load_scale_planes(nc, b_planes, B_scales)
         load_word_chunk(nc, b_words, B_words, 0)
         load_x(2)
-        nc.sync.dma_start(out=s2_all[:], in_=scaling2.partition_broadcast(P))
         load_x(3)
         for c in range(1, CHUNKS):
             load_word_chunk(nc, b_words, B_words, c)
@@ -170,7 +174,15 @@ def tile_doublebinarylinear_kernel(
             adder.tensor_tensor(out=result[:], in0=result[:], in1=bias_all[:, cols], op=ADD)
             nc.sync.dma_start(out=out_rows[rows, cols], in_=result[:])
 
+        def spread_s2(c):
+            cols = slice(c * N_TILE, (c + 1) * N_TILE)
+            acc = psum.tile([P, N_TILE], F32, tag="acc", bufs=5)
+            nc.tensor.matmul(acc[:], lhsT=ones[:], rhs=s2_row[:, cols], start=True, stop=True)
+            nc.scalar.copy(out=s2_all[:, cols], in_=acc[:])
+
         quantise_x(0)
+        for c in range(CHUNKS):
+            spread_s2(c)
         quantise_x(1)
         first_product(0, 0)
         quantise_x(2)

@@ -25,11 +25,11 @@ WORDS_PER_PASS = K_PASS // 2
 FLOPS = 2 * 2 * TOKENS * DIM * DIM
 
 
-def load_scale_planes(nc, planes, scales):
+def load_scale_planes(nc, planes, scales, cols):
     for quadrant in range(QUADRANTS):
         nc.sync.dma_start(
-            out=planes[32 * quadrant : 32 * quadrant + 4 * PASSES, :].bitcast(I32),
-            in_=scales[:, 4 * quadrant : 4 * quadrant + 4, :].bitcast(I32),
+            out=planes[32 * quadrant : 32 * quadrant + 4 * PASSES, cols].bitcast(I32),
+            in_=scales[:, 4 * quadrant : 4 * quadrant + 4, cols].bitcast(I32),
         )
 
 
@@ -79,28 +79,36 @@ def tile_doublebinarylinear_kernel(
         h2_scales = keep.tile([P, PASSES, TOKENS], U8, align_bytes=64)
         ident_f32 = keep.tile([P, P], F32)
         ones = keep.tile([P, P], BF16)
+        warm = keep.tile([P, N_TILE], BF16)
+        ident_bf16 = keep.tile([P, P], BF16)
+        s0_rows = keep.tile([P, K_PASS], BF16)
         s2_row = keep.tile([P, DIM], BF16)
 
-        nc.vector.memset(s2_row[:].bitcast(I32), 0)
         nc.vector.memset(ones[:], 1.0)
+        nc.vector.memset(warm[:].bitcast(I32), 0)
+        nc.vector.memset(s0_rows[:].bitcast(I32), 0)
+        nc.vector.memset(s2_row[:].bitcast(I32), 0)
         nc.vector.memset(b_planes[:].bitcast(I32), 0)
         nc.vector.memset(a_planes[:].bitcast(I32), 0)
+        make_identity(nc, ident_bf16[:])
         make_identity(nc, ident_f32[:])
 
         def load_x(i):
             nc.sync.dma_start(out=x_sb[:, i, :], in_=x_rows[i * P : (i + 1) * P, :])
 
-        nc.sync.dma_start(out=s0_by_k[:], in_=scaling0.rearrange("(g p t) -> p g t", g=PASSES, p=P))
-        load_x(0)
+        nc.sync.dma_start(out=x_sb[:, 0, 0 : DIM // 2], in_=x_rows[0:P, 0 : DIM // 2])
+        nc.sync.dma_start(out=s0_rows[0:PASSES, :], in_=scaling0.rearrange("(g k) -> g k", g=PASSES))
+        nc.sync.dma_start(out=x_sb[:, 0, DIM // 2 : DIM], in_=x_rows[0:P, DIM // 2 : DIM])
         nc.sync.dma_start(out=s2_row[0:1, :], in_=scaling2.rearrange("(o n) -> o n", o=1))
         load_x(1)
-        load_scale_planes(nc, b_planes, B_scales)
+        load_scale_planes(nc, b_planes, B_scales, slice(0, N_TILE))
         load_word_chunk(nc, b_words, B_words, 0)
         load_x(2)
         load_x(3)
+        load_scale_planes(nc, b_planes, B_scales, slice(N_TILE, DIM))
         for c in range(1, CHUNKS):
             load_word_chunk(nc, b_words, B_words, c)
-        load_scale_planes(nc, a_planes, A_scales)
+        load_scale_planes(nc, a_planes, A_scales, slice(0, DIM))
         load_word_chunk(nc, a_words, A_words, 0)
         nc.sync.dma_start(out=s4_all[:], in_=scaling4.partition_broadcast(P))
         nc.sync.dma_start(out=bias_all[:], in_=bias.partition_broadcast(P))
@@ -163,16 +171,24 @@ def tile_doublebinarylinear_kernel(
                 in_=h2_by_k[:].rearrange("p j r t -> p (j r t)"),
             )
 
-        def second_product(i, c):
+        results = []
+
+        def second_product(i, first_col, width, adder):
             rows = slice(i * P, (i + 1) * P)
-            cols = slice(c * N_TILE, (c + 1) * N_TILE)
+            cols = slice(first_col, first_col + width)
             acc = psum.tile([P, N_TILE], F32, tag="acc", bufs=5)
-            mx_output_tile(nc, acc[:], h2_words[:, :, rows], h2_scales[:, :, rows], a_words, a_planes, cols)
-            result = work.tile([P, N_TILE], F32, bufs=4)
-            nc.vector.tensor_tensor(out=result[:], in0=acc[:], in1=s4_all[:, cols], op=MULT)
-            adder = nc.gpsimd if i % 2 == 0 else nc.vector
-            adder.tensor_tensor(out=result[:], in0=result[:], in1=bias_all[:, cols], op=ADD)
-            nc.sync.dma_start(out=out_rows[rows, cols], in_=result[:])
+            mx_output_tile(nc, acc[:, 0:width], h2_words[:, :, rows], h2_scales[:, :, rows], a_words, a_planes, cols)
+            result = work.tile([P, N_TILE], F32, bufs=6)
+            nc.vector.tensor_tensor(out=result[:, 0:width], in0=acc[:, 0:width], in1=s4_all[:, cols], op=MULT)
+            if results:
+                finish_result()
+            results.append((result, rows, cols, adder))
+
+        def finish_result():
+            result, rows, cols, adder = results.pop(0)
+            done = result[:, 0 : cols.stop - cols.start]
+            adder.tensor_tensor(out=done, in0=done, in1=bias_all[:, cols], op=ADD)
+            nc.sync.dma_start(out=out_rows[rows, cols], in_=done)
 
         def spread_s2(c):
             cols = slice(c * N_TILE, (c + 1) * N_TILE)
@@ -180,6 +196,19 @@ def tile_doublebinarylinear_kernel(
             nc.tensor.matmul(acc[:], lhsT=ones[:], rhs=s2_row[:, cols], start=True, stop=True)
             nc.scalar.copy(out=s2_all[:, cols], in_=acc[:])
 
+        def turn_s0():
+            s0_t = psum.tile([P, PACK, P], BF16, tag="transposed", bufs=3)
+            for t in range(PACK):
+                nc.tensor.transpose(s0_t[:, t, :], s0_rows[:, t:K_PASS:PACK], ident_bf16[:])
+            nc.scalar.copy(out=s0_by_k[:], in_=s0_t[:, :, 0:PASSES].rearrange("p t g -> p g t"))
+
+        def warm_up(count):
+            acc = psum.tile([P, N_TILE], F32, tag="acc", bufs=5)
+            for n in range(count):
+                nc.tensor.matmul(acc[:], lhsT=ones[:], rhs=warm[:], start=True, stop=True)
+
+        warm_up(6)
+        turn_s0()
         quantise_x(0)
         for c in range(CHUNKS):
             spread_s2(c)
@@ -198,10 +227,16 @@ def tile_doublebinarylinear_kernel(
             if c == CHUNKS - 1:
                 quantise_h2(0, c)
             first_product(3, c)
-        second_product(0, 0)
-        quantise_h2(1, CHUNKS - 1)
-        for i in range(1, TOKEN_TILES):
-            second_product(i, 0)
-        for c in range(1, CHUNKS):
+        def adder_of(i, c):
+            return nc.gpsimd if i % 2 == 0 and c < CHUNKS - 1 else nc.vector
+
+        for c in range(CHUNKS):
             for i in range(TOKEN_TILES):
-                second_product(i, c)
+                if (i, c) == (TOKEN_TILES - 1, CHUNKS - 1):
+                    for first_col in (c * N_TILE, c * N_TILE + N_TILE // 2):
+                        second_product(i, first_col, N_TILE // 2, nc.vector)
+                else:
+                    second_product(i, c * N_TILE, N_TILE, adder_of(i, c))
+                if (i, c) == (0, 0):
+                    quantise_h2(1, CHUNKS - 1)
+        finish_result()

@@ -117,15 +117,20 @@ def tile_doublebinarylinear_kernel(
 
         def quantise_x(i):
             x_pairs = x_sb[:, i, :].bitcast(F32)
+            if i > 0:
+                x_split = work.tile([P, PASSES, 2, P], F32)
+                nc.scalar.copy(out=x_split[:], in_=x_pairs.rearrange("r (g p u) -> r g u p", g=PASSES, u=2))
             h0 = work.tile([P, PASSES, P, PACK], BF16, align_bytes=64)
             for half in range(PASSES // 2):
                 pairs_t = psum.tile([P, 2, 2, P], F32, tag="transposed", bufs=3)
                 for gg in range(2):
                     first = (2 * half + gg) * WORDS_PER_PASS
                     for u in range(2):
-                        nc.tensor.transpose(
-                            pairs_t[:, gg, u, :], x_pairs[:, first + u : first + WORDS_PER_PASS : 2], ident_f32[:]
-                        )
+                        if i > 0:
+                            words = x_split[:, 2 * half + gg, u, :]
+                        else:
+                            words = x_pairs[:, first + u : first + WORDS_PER_PASS : 2]
+                        nc.tensor.transpose(pairs_t[:, gg, u, :], words, ident_f32[:])
                 for gg in range(2):
                     g = 2 * half + gg
                     x_t = pairs_t[:, gg].rearrange("p u r -> p (u r)").bitcast(BF16)
@@ -218,17 +223,21 @@ def tile_doublebinarylinear_kernel(
         quantise_x(3)
         for i in range(1, TOKEN_TILES):
             first_product(i, 0)
-        for c in range(1, CHUNKS):
+        for c in range(1, CHUNKS - 1):
             first_product(0, c)
             first_product(1, c)
             quantise_h2(0, c - 1)
             quantise_h2(1, c - 1)
             first_product(2, c)
-            if c == CHUNKS - 1:
-                quantise_h2(0, c)
             first_product(3, c)
+        for i in range(TOKEN_TILES - 1):
+            first_product(i, CHUNKS - 1)
+        quantise_h2(0, CHUNKS - 2)
+        quantise_h2(1, CHUNKS - 2)
+        quantise_h2(0, CHUNKS - 1)
+        first_product(TOKEN_TILES - 1, CHUNKS - 1)
         def adder_of(i, c):
-            return nc.gpsimd if i % 2 == 0 and c < CHUNKS - 1 else nc.vector
+            return nc.gpsimd if i % 2 == 0 and (i, c) != (2, CHUNKS - 1) else nc.vector
 
         for c in range(CHUNKS):
             for i in range(TOKEN_TILES):

@@ -22,6 +22,8 @@ CHUNKS = DIM // N_TILE
 QUADRANTS = 4
 WORDS_PER_PASS = K_PASS // 2
 
+LAID_OUT_TILES = (2, 3)
+
 FLOPS = 2 * 2 * TOKENS * DIM * DIM
 
 
@@ -117,7 +119,7 @@ def tile_doublebinarylinear_kernel(
 
         def quantise_x(i):
             x_pairs = x_sb[:, i, :].bitcast(F32)
-            if i > 0:
+            if i in LAID_OUT_TILES:
                 x_split = work.tile([P, PASSES, 2, P], F32)
                 nc.scalar.copy(out=x_split[:], in_=x_pairs.rearrange("r (g p u) -> r g u p", g=PASSES, u=2))
             h0 = work.tile([P, PASSES, P, PACK], BF16, align_bytes=64)
@@ -126,7 +128,7 @@ def tile_doublebinarylinear_kernel(
                 for gg in range(2):
                     first = (2 * half + gg) * WORDS_PER_PASS
                     for u in range(2):
-                        if i > 0:
+                        if i in LAID_OUT_TILES:
                             words = x_split[:, 2 * half + gg, u, :]
                         else:
                             words = x_pairs[:, first + u : first + WORDS_PER_PASS : 2]
@@ -219,11 +221,18 @@ def tile_doublebinarylinear_kernel(
             spread_s2(c)
         quantise_x(1)
         first_product(0, 0)
+        first_product(1, 0)
         quantise_x(2)
         quantise_x(3)
-        for i in range(1, TOKEN_TILES):
-            first_product(i, 0)
-        for c in range(1, CHUNKS - 1):
+        first_product(2, 0)
+        first_product(0, 1)
+        first_product(3, 0)
+        first_product(1, 1)
+        quantise_h2(0, 0)
+        quantise_h2(1, 0)
+        first_product(2, 1)
+        first_product(3, 1)
+        for c in range(2, CHUNKS - 1):
             first_product(0, c)
             first_product(1, c)
             quantise_h2(0, c - 1)
@@ -248,4 +257,6 @@ def tile_doublebinarylinear_kernel(
                     second_product(i, c * N_TILE, N_TILE, adder_of(i, c))
                 if (i, c) == (0, 0):
                     quantise_h2(1, CHUNKS - 1)
+                if (i, c) == (1, CHUNKS - 1):
+                    finish_result()
         finish_result()

@@ -180,7 +180,7 @@ def tile_doublebinarylinear_kernel(
 
         results = []
 
-        def second_product(i, first_col, width, adder):
+        def second_product(i, first_col, width):
             rows = slice(i * P, (i + 1) * P)
             cols = slice(first_col, first_col + width)
             acc = psum.tile([P, N_TILE], F32, tag="acc", bufs=5)
@@ -189,12 +189,12 @@ def tile_doublebinarylinear_kernel(
             nc.vector.tensor_tensor(out=result[:, 0:width], in0=acc[:, 0:width], in1=s4_all[:, cols], op=MULT)
             if results:
                 finish_result()
-            results.append((result, rows, cols, adder))
+            results.append((result, rows, cols))
 
         def finish_result():
-            result, rows, cols, adder = results.pop(0)
+            result, rows, cols = results.pop(0)
             done = result[:, 0 : cols.stop - cols.start]
-            adder.tensor_tensor(out=done, in0=done, in1=bias_all[:, cols], op=ADD)
+            nc.vector.tensor_tensor(out=done, in0=done, in1=bias_all[:, cols], op=ADD)
             nc.sync.dma_start(out=out_rows[rows, cols], in_=done)
 
         def spread_s2(c):
@@ -220,6 +220,7 @@ def tile_doublebinarylinear_kernel(
         for c in range(CHUNKS):
             spread_s2(c)
         quantise_x(1)
+        warm_up(4)
         first_product(0, 0)
         first_product(1, 0)
         quantise_x(2)
@@ -245,16 +246,13 @@ def tile_doublebinarylinear_kernel(
         quantise_h2(1, CHUNKS - 2)
         quantise_h2(0, CHUNKS - 1)
         first_product(TOKEN_TILES - 1, CHUNKS - 1)
-        def adder_of(i, c):
-            return nc.gpsimd if i % 2 == 0 and (i, c) != (2, CHUNKS - 1) else nc.vector
-
         for c in range(CHUNKS):
             for i in range(TOKEN_TILES):
                 if (i, c) == (TOKEN_TILES - 1, CHUNKS - 1):
                     for first_col in (c * N_TILE, c * N_TILE + N_TILE // 2):
-                        second_product(i, first_col, N_TILE // 2, nc.vector)
+                        second_product(i, first_col, N_TILE // 2)
                 else:
-                    second_product(i, c * N_TILE, N_TILE, adder_of(i, c))
+                    second_product(i, c * N_TILE, N_TILE)
                 if (i, c) == (0, 0):
                     quantise_h2(1, CHUNKS - 1)
                 if (i, c) == (1, CHUNKS - 1):

@@ -142,11 +142,13 @@ def tile_doublebinarylinear_kernel(
                         in1=s0_by_k[:, g].rearrange("p (u e) -> p u e", u=2).unsqueeze(1).to_broadcast([P, P, 2, 2]),
                         op=MULT,
                     )
-            nc.vector.quantize_mx(
-                out=h0_words[:, i].rearrange("p g r -> p (g r)").bitcast(FP8X4),
-                scales=h0_scales[:, i].rearrange("p g r -> p (g r)"),
-                in_=h0[:].rearrange("p g r t -> p (g r t)"),
-            )
+            for half in range(PASSES // 2):
+                passes = slice(2 * half, 2 * half + 2)
+                nc.vector.quantize_mx(
+                    out=h0_words[:, i, passes].rearrange("p g r -> p (g r)").bitcast(FP8X4),
+                    scales=h0_scales[:, i, passes].rearrange("p g r -> p (g r)"),
+                    in_=h0[:, passes].rearrange("p g r t -> p (g r t)"),
+                )
 
         h2_tiles = {}
 

@@ -21,8 +21,8 @@ N_TILE = 512
 CHUNKS = DIM // N_TILE
 QUADRANTS = 4
 WORDS_PER_PASS = K_PASS // 2
-
-LAID_OUT_TILES = (2, 3)
+TOKEN_PAIRS = TOKEN_TILES // 2
+PAIR = 2 * P
 
 FLOPS = 2 * 2 * TOKENS * DIM * DIM
 
@@ -43,17 +43,16 @@ def load_word_chunk(nc, words, words_dram, chunk):
     )
 
 
-def mx_output_tile(nc, acc, act_words, act_scales, weight_words, weight_planes, cols):
-    for g in range(PASSES):
-        nc.tensor.matmul_mx(
-            out=acc,
-            lhsT=act_words[:, g, :].bitcast(FP8X4),
-            lhsT_scale=act_scales[:, g, :],
-            rhs=weight_words[:, g, cols].bitcast(FP8X4),
-            rhs_scale=weight_planes[4 * g : P, cols],
-            start=(g == 0),
-            stop=(g == PASSES - 1),
-        )
+def mx_pass(nc, acc, act_words, act_scales, rows, weight_words, weight_planes, cols, g):
+    nc.tensor.matmul_mx(
+        out=acc,
+        lhsT=act_words[:, g, rows].bitcast(FP8X4),
+        lhsT_scale=act_scales[:, g, rows],
+        rhs=weight_words[:, g, cols].bitcast(FP8X4),
+        rhs_scale=weight_planes[4 * g : P, cols],
+        start=(g == 0),
+        stop=(g == PASSES - 1),
+    )
 
 
 def tile_doublebinarylinear_kernel(
@@ -66,7 +65,7 @@ def tile_doublebinarylinear_kernel(
     with tc.tile_pool(name="keep", bufs=1) as keep, tc.tile_pool(name="work", bufs=2) as work, tc.psum_pool(
         name="psum", bufs=1
     ) as psum, tc.manual_schedule():
-        x_sb = keep.tile([P, TOKEN_TILES, DIM], BF16)
+        x_sb = keep.tile([P, PASSES, TOKEN_TILES, K_PASS], BF16)
         s0_by_k = keep.tile([P, PASSES, PACK], BF16)
         s2_all = keep.tile([P, DIM], BF16)
         s4_all = keep.tile([P, DIM], BF16)
@@ -75,8 +74,8 @@ def tile_doublebinarylinear_kernel(
         a_words = keep.tile([P, PASSES, DIM], U32, align_bytes=64)
         b_planes = keep.tile([P, DIM], U8, align_bytes=64)
         a_planes = keep.tile([P, DIM], U8, align_bytes=64)
-        h0_words = keep.tile([P, TOKEN_TILES, PASSES, P], U32, align_bytes=64)
-        h0_scales = keep.tile([P, TOKEN_TILES, PASSES, P], U8, align_bytes=64)
+        h0_words = keep.tile([P, PASSES, TOKENS], U32, align_bytes=64)
+        h0_scales = keep.tile([P, PASSES, TOKENS], U8, align_bytes=64)
         h2_words = keep.tile([P, PASSES, TOKENS], U32, align_bytes=64)
         h2_scales = keep.tile([P, PASSES, TOKENS], U8, align_bytes=64)
         ident_f32 = keep.tile([P, P], F32)
@@ -89,24 +88,36 @@ def tile_doublebinarylinear_kernel(
         nc.vector.memset(ones[:], 1.0)
         nc.vector.memset(warm[:].bitcast(I32), 0)
         nc.vector.memset(s0_rows[:].bitcast(I32), 0)
-        nc.vector.memset(s2_row[:].bitcast(I32), 0)
         nc.vector.memset(b_planes[:].bitcast(I32), 0)
+        nc.vector.memset(s2_row[:].bitcast(I32), 0)
         nc.vector.memset(a_planes[:].bitcast(I32), 0)
         make_identity(nc, ident_bf16[:])
         make_identity(nc, ident_f32[:])
 
-        def load_x(i):
-            nc.sync.dma_start(out=x_sb[:, i, :], in_=x_rows[i * P : (i + 1) * P, :])
+        x_by_tile = x_rows.rearrange("(i p) k -> p i k", p=P)
 
-        nc.sync.dma_start(out=x_sb[:, 0, 0 : DIM // 2], in_=x_rows[0:P, 0 : DIM // 2])
+        def load_x(g, tiles):
+            ks = slice(g * K_PASS, (g + 1) * K_PASS)
+            nc.sync.dma_start(out=x_sb[:, g, tiles, :], in_=x_by_tile[:, tiles, ks])
+
+        def load_word_pass(g):
+            byte_cols = slice(0, N_TILE * PACK)
+            nc.sync.dma_start(
+                out=b_words[:, g, 0:N_TILE].bitcast(I32),
+                in_=B_words[g].rearrange("p n t -> p (n t)")[:, byte_cols].bitcast(I32),
+            )
+
+        load_x(0, slice(0, 2))
+        load_x(0, slice(2, 4))
         nc.sync.dma_start(out=s0_rows[0:PASSES, :], in_=scaling0.rearrange("(g k) -> g k", g=PASSES))
-        nc.sync.dma_start(out=x_sb[:, 0, DIM // 2 : DIM], in_=x_rows[0:P, DIM // 2 : DIM])
-        nc.sync.dma_start(out=s2_row[0:1, :], in_=scaling2.rearrange("(o n) -> o n", o=1))
-        load_x(1)
         load_scale_planes(nc, b_planes, B_scales, slice(0, N_TILE))
-        load_word_chunk(nc, b_words, B_words, 0)
-        load_x(2)
-        load_x(3)
+        load_word_pass(0)
+        nc.sync.dma_start(out=s2_row[0:1, :], in_=scaling2.rearrange("(o n) -> o n", o=1))
+        load_x(1, slice(0, 4))
+        load_word_pass(1)
+        for g in range(2, PASSES):
+            load_x(g, slice(0, 4))
+            load_word_pass(g)
         load_scale_planes(nc, b_planes, B_scales, slice(N_TILE, DIM))
         for c in range(1, CHUNKS):
             load_word_chunk(nc, b_words, B_words, c)
@@ -117,45 +128,45 @@ def tile_doublebinarylinear_kernel(
         for c in range(1, CHUNKS):
             load_word_chunk(nc, a_words, A_words, c)
 
-        def quantise_x(i):
-            x_pairs = x_sb[:, i, :].bitcast(F32)
-            if i in LAID_OUT_TILES:
-                x_split = work.tile([P, PASSES, 2, P], F32)
-                nc.scalar.copy(out=x_split[:], in_=x_pairs.rearrange("r (g p u) -> r g u p", g=PASSES, u=2))
-            h0 = work.tile([P, PASSES, P, PACK], BF16, align_bytes=64)
-            for half in range(PASSES // 2):
+        def quantise_x(g):
+            h0 = work.tile([P, TOKENS, PACK], BF16, align_bytes=64)
+            for pair in range(TOKEN_PAIRS):
+                rows = slice(pair * PAIR, (pair + 1) * PAIR)
                 pairs_t = psum.tile([P, 2, 2, P], F32, tag="transposed", bufs=3)
-                for gg in range(2):
-                    first = (2 * half + gg) * WORDS_PER_PASS
+                for j in range(2):
+                    x_words = x_sb[:, g, 2 * pair + j, :].bitcast(F32)
                     for u in range(2):
-                        if i in LAID_OUT_TILES:
-                            words = x_split[:, 2 * half + gg, u, :]
-                        else:
-                            words = x_pairs[:, first + u : first + WORDS_PER_PASS : 2]
-                        nc.tensor.transpose(pairs_t[:, gg, u, :], words, ident_f32[:])
-                for gg in range(2):
-                    g = 2 * half + gg
-                    x_t = pairs_t[:, gg].rearrange("p u r -> p (u r)").bitcast(BF16)
-                    nc.vector.tensor_tensor(
-                        out=h0[:, g].rearrange("p r (u e) -> p r u e", u=2),
-                        in0=x_t.rearrange("p (u r e) -> p r u e", u=2, e=2),
-                        in1=s0_by_k[:, g].rearrange("p (u e) -> p u e", u=2).unsqueeze(1).to_broadcast([P, P, 2, 2]),
-                        op=MULT,
-                    )
-            for half in range(PASSES // 2):
-                passes = slice(2 * half, 2 * half + 2)
+                        nc.tensor.transpose(pairs_t[:, u, j, :], x_words[:, u:WORDS_PER_PASS:2], ident_f32[:])
+                x_t = pairs_t[:].rearrange("p u j r -> p (u j r)").bitcast(BF16)
+                nc.vector.tensor_tensor(
+                    out=h0[:, rows].rearrange("p r (u e) -> p r u e", u=2),
+                    in0=x_t.rearrange("p (u r e) -> p r u e", u=2, e=2),
+                    in1=s0_by_k[:, g].rearrange("p (u e) -> p u e", u=2).unsqueeze(1).to_broadcast([P, PAIR, 2, 2]),
+                    op=MULT,
+                )
+            for pair in range(TOKEN_PAIRS):
+                rows = slice(pair * PAIR, (pair + 1) * PAIR)
                 nc.vector.quantize_mx(
-                    out=h0_words[:, i, passes].rearrange("p g r -> p (g r)").bitcast(FP8X4),
-                    scales=h0_scales[:, i, passes].rearrange("p g r -> p (g r)"),
-                    in_=h0[:, passes].rearrange("p g r t -> p (g r t)"),
+                    out=h0_words[:, g, rows].bitcast(FP8X4),
+                    scales=h0_scales[:, g, rows],
+                    in_=h0[:, rows].rearrange("p r t -> p (r t)"),
                 )
 
         h2_tiles = {}
 
-        def first_product(i, c):
+        def first_pass(acc, i, c, g):
+            rows = slice(i * P, (i + 1) * P)
             cols = slice(c * N_TILE, (c + 1) * N_TILE)
+            mx_pass(nc, acc[:], h0_words, h0_scales, rows, b_words, b_planes, cols, g)
+
+        def first_product(i, c):
             acc = psum.tile([P, N_TILE], F32, tag="acc", bufs=5)
-            mx_output_tile(nc, acc[:], h0_words[:, i], h0_scales[:, i], b_words, b_planes, cols)
+            for g in range(PASSES):
+                first_pass(acc, i, c, g)
+            scale_by_s2(acc, i, c)
+
+        def scale_by_s2(acc, i, c):
+            cols = slice(c * N_TILE, (c + 1) * N_TILE)
             h2 = work.tile([P, 2, P, 2], BF16, bufs=8)
             nc.vector.tensor_tensor(
                 out=h2[:],
@@ -186,7 +197,8 @@ def tile_doublebinarylinear_kernel(
             rows = slice(i * P, (i + 1) * P)
             cols = slice(first_col, first_col + width)
             acc = psum.tile([P, N_TILE], F32, tag="acc", bufs=5)
-            mx_output_tile(nc, acc[:, 0:width], h2_words[:, :, rows], h2_scales[:, :, rows], a_words, a_planes, cols)
+            for g in range(PASSES):
+                mx_pass(nc, acc[:, 0:width], h2_words, h2_scales, rows, a_words, a_planes, cols, g)
             result = work.tile([P, N_TILE], F32, bufs=6)
             nc.vector.tensor_tensor(out=result[:, 0:width], in0=acc[:, 0:width], in1=s4_all[:, cols], op=MULT)
             if results:
@@ -222,20 +234,18 @@ def tile_doublebinarylinear_kernel(
         for c in range(CHUNKS):
             spread_s2(c)
         quantise_x(1)
-        warm_up(4)
-        first_product(0, 0)
-        first_product(1, 0)
-        quantise_x(2)
-        quantise_x(3)
-        first_product(2, 0)
-        first_product(0, 1)
-        first_product(3, 0)
-        first_product(1, 1)
-        quantise_h2(0, 0)
-        quantise_h2(1, 0)
-        first_product(2, 1)
-        first_product(3, 1)
-        for c in range(2, CHUNKS - 1):
+        accs = []
+        for i in range(TOKEN_TILES):
+            acc = psum.tile([P, N_TILE], F32, tag="acc", bufs=5)
+            accs.append(acc)
+        for g in range(PASSES):
+            for i in range(TOKEN_TILES):
+                first_pass(accs[i], i, 0, g)
+                if g == PASSES - 1:
+                    scale_by_s2(accs[i], i, 0)
+            if g + 2 < PASSES:
+                quantise_x(g + 2)
+        for c in range(1, CHUNKS - 1):
             first_product(0, c)
             first_product(1, c)
             quantise_h2(0, c - 1)

@@ -9,6 +9,7 @@ U8 = mybir.dt.uint8
 FP8X4 = mybir.dt.float8_e4m3fn_x4
 MULT = mybir.AluOpType.mult
 ADD = mybir.AluOpType.add
+COPY = mybir.ActivationFunctionType.Copy
 
 P = 128
 PACK = 4
@@ -19,10 +20,12 @@ TOKEN_TILES = TOKENS // P
 PASSES = DIM // K_PASS
 N_TILE = 512
 CHUNKS = DIM // N_TILE
+LANES = N_TILE // PACK
 QUADRANTS = 4
 WORDS_PER_PASS = K_PASS // 2
 TOKEN_PAIRS = TOKEN_TILES // 2
 PAIR = 2 * P
+HALVES = (slice(0, PAIR), slice(PAIR, TOKENS))
 
 FLOPS = 2 * 2 * TOKENS * DIM * DIM
 
@@ -38,20 +41,8 @@ def load_scale_planes(nc, planes, scales, cols):
 def load_word_chunk(nc, words, words_dram, chunk):
     byte_cols = slice(chunk * N_TILE * PACK, (chunk + 1) * N_TILE * PACK)
     nc.sync.dma_start(
-        out=words[:, :, chunk * N_TILE : (chunk + 1) * N_TILE].bitcast(I32),
+        out=words[:, chunk].bitcast(I32),
         in_=words_dram.rearrange("g p n t -> p g (n t)")[:, :, byte_cols].bitcast(I32),
-    )
-
-
-def mx_pass(nc, acc, act_words, act_scales, rows, weight_words, weight_planes, cols, g):
-    nc.tensor.matmul_mx(
-        out=acc,
-        lhsT=act_words[:, g, rows].bitcast(FP8X4),
-        lhsT_scale=act_scales[:, g, rows],
-        rhs=weight_words[:, g, cols].bitcast(FP8X4),
-        rhs_scale=weight_planes[4 * g : P, cols],
-        start=(g == 0),
-        stop=(g == PASSES - 1),
     )
 
 
@@ -66,30 +57,30 @@ def tile_doublebinarylinear_kernel(
         name="psum", bufs=1
     ) as psum, tc.manual_schedule():
         x_sb = keep.tile([P, PASSES, TOKEN_TILES, K_PASS], BF16)
+        s_rows = keep.tile([P, K_PASS], BF16)
         s0_by_k = keep.tile([P, PASSES, PACK], BF16)
-        s2_all = keep.tile([P, DIM], BF16)
+        s2_by_k = keep.tile([P, CHUNKS, PACK], F32)
         s4_all = keep.tile([P, DIM], BF16)
         bias_all = keep.tile([P, DIM], BF16)
-        b_words = keep.tile([P, PASSES, DIM], U32, align_bytes=64)
-        a_words = keep.tile([P, PASSES, DIM], U32, align_bytes=64)
-        b_planes = keep.tile([P, DIM], U8, align_bytes=64)
+        b_loaded = keep.tile([P, CHUNKS, PASSES, N_TILE], U32, align_bytes=64)
+        b_planes_loaded = keep.tile([P, DIM], U8, align_bytes=64)
+        b_words = keep.tile([P, CHUNKS, PASSES, PACK, LANES], U32, align_bytes=64)
+        b_planes = keep.tile([P, CHUNKS, PACK, LANES], U8, align_bytes=64)
+        a_words = keep.tile([P, CHUNKS, PASSES, N_TILE], U32, align_bytes=64)
         a_planes = keep.tile([P, DIM], U8, align_bytes=64)
         h0_words = keep.tile([P, PASSES, TOKENS], U32, align_bytes=64)
         h0_scales = keep.tile([P, PASSES, TOKENS], U8, align_bytes=64)
         h2_words = keep.tile([P, PASSES, TOKENS], U32, align_bytes=64)
         h2_scales = keep.tile([P, PASSES, TOKENS], U8, align_bytes=64)
         ident_f32 = keep.tile([P, P], F32)
+        ident_bf16 = keep.tile([P, P], BF16)
         ones = keep.tile([P, P], BF16)
         warm = keep.tile([P, N_TILE], BF16)
-        ident_bf16 = keep.tile([P, P], BF16)
-        s0_rows = keep.tile([P, K_PASS], BF16)
-        s2_row = keep.tile([P, DIM], BF16)
 
         nc.vector.memset(ones[:], 1.0)
         nc.vector.memset(warm[:].bitcast(I32), 0)
-        nc.vector.memset(s0_rows[:].bitcast(I32), 0)
-        nc.vector.memset(b_planes[:].bitcast(I32), 0)
-        nc.vector.memset(s2_row[:].bitcast(I32), 0)
+        nc.vector.memset(s_rows[:].bitcast(I32), 0)
+        nc.vector.memset(b_planes_loaded[:].bitcast(I32), 0)
         nc.vector.memset(a_planes[:].bitcast(I32), 0)
         make_identity(nc, ident_bf16[:])
         make_identity(nc, ident_f32[:])
@@ -103,29 +94,32 @@ def tile_doublebinarylinear_kernel(
         def load_word_pass(g):
             byte_cols = slice(0, N_TILE * PACK)
             nc.sync.dma_start(
-                out=b_words[:, g, 0:N_TILE].bitcast(I32),
+                out=b_loaded[:, 0, g].bitcast(I32),
                 in_=B_words[g].rearrange("p n t -> p (n t)")[:, byte_cols].bitcast(I32),
             )
 
         load_x(0, slice(0, 2))
         load_x(0, slice(2, 4))
-        nc.sync.dma_start(out=s0_rows[0:PASSES, :], in_=scaling0.rearrange("(g k) -> g k", g=PASSES))
-        load_scale_planes(nc, b_planes, B_scales, slice(0, N_TILE))
+        nc.sync.dma_start(out=s_rows[0:PASSES, :], in_=scaling0.rearrange("(g k) -> g k", g=PASSES))
+        nc.sync.dma_start(
+            out=s_rows[PASSES : PASSES + CHUNKS, :], in_=scaling2.rearrange("(c k) -> c k", c=CHUNKS)
+        )
+        load_scale_planes(nc, b_planes_loaded, B_scales, slice(0, N_TILE))
         load_word_pass(0)
-        nc.sync.dma_start(out=s2_row[0:1, :], in_=scaling2.rearrange("(o n) -> o n", o=1))
         load_x(1, slice(0, 4))
         load_word_pass(1)
         for g in range(2, PASSES):
             load_x(g, slice(0, 4))
             load_word_pass(g)
-        load_scale_planes(nc, b_planes, B_scales, slice(N_TILE, DIM))
+        load_scale_planes(nc, b_planes_loaded, B_scales, slice(N_TILE, DIM))
         for c in range(1, CHUNKS):
-            load_word_chunk(nc, b_words, B_words, c)
+            load_word_chunk(nc, b_loaded, B_words, c)
         load_scale_planes(nc, a_planes, A_scales, slice(0, DIM))
-        load_word_chunk(nc, a_words, A_words, 0)
+        for c in range(2):
+            load_word_chunk(nc, a_words, A_words, c)
         nc.sync.dma_start(out=s4_all[:], in_=scaling4.partition_broadcast(P))
         nc.sync.dma_start(out=bias_all[:], in_=bias.partition_broadcast(P))
-        for c in range(1, CHUNKS):
+        for c in range(2, CHUNKS):
             load_word_chunk(nc, a_words, A_words, c)
 
         def quantise_x(g):
@@ -152,53 +146,73 @@ def tile_doublebinarylinear_kernel(
                     in_=h0[:, rows].rearrange("p r t -> p (r t)"),
                 )
 
-        h2_tiles = {}
-
-        def first_pass(acc, i, c, g):
-            rows = slice(i * P, (i + 1) * P)
-            cols = slice(c * N_TILE, (c + 1) * N_TILE)
-            mx_pass(nc, acc[:], h0_words, h0_scales, rows, b_words, b_planes, cols, g)
-
-        def first_product(i, c):
-            acc = psum.tile([P, N_TILE], F32, tag="acc", bufs=5)
-            for g in range(PASSES):
-                first_pass(acc, i, c, g)
-            scale_by_s2(acc, i, c)
-
-        def scale_by_s2(acc, i, c):
-            cols = slice(c * N_TILE, (c + 1) * N_TILE)
-            h2 = work.tile([P, 2, P, 2], BF16, bufs=8)
-            nc.vector.tensor_tensor(
-                out=h2[:],
-                in0=acc[:].rearrange("r (p u e) -> r u p e", u=2, e=2),
-                in1=s2_all[:, cols].rearrange("r (p u e) -> r u p e", u=2, e=2),
-                op=MULT,
+        def order_b_words(c, passes):
+            nc.vector.tensor_copy(
+                out=b_words[:, c, passes].bitcast(I32),
+                in_=b_loaded[:, c, passes].bitcast(I32).rearrange("p g (m t) -> p g t m", t=PACK),
             )
-            h2_tiles[i, c] = h2
 
-        def quantise_h2(pair, c):
-            rows = slice(pair * 2 * P, (pair + 1) * 2 * P)
-            h2_t = psum.tile([P, 2, 2, P], F32, tag="transposed", bufs=3)
-            for j in range(2):
-                for u in range(2):
-                    h2_words_u = h2_tiles[2 * pair + j, c][:, u].rearrange("r p e -> r (p e)").bitcast(F32)
-                    nc.tensor.transpose(h2_t[:, j, u, :], h2_words_u, ident_f32[:])
-            h2_by_k = work.tile([P, 2, P, PACK], BF16, bufs=3, align_bytes=64)
-            nc.scalar.copy(out=h2_by_k[:].bitcast(F32), in_=h2_t[:].rearrange("p j u r -> p j r u"))
+        def order_b_planes(c):
+            cols = slice(c * N_TILE, (c + 1) * N_TILE)
+            nc.vector.tensor_copy(
+                out=b_planes[:, c], in_=b_planes_loaded[:, cols].rearrange("p (m t) -> p t m", t=PACK)
+            )
+
+        def first_pass(out, c, t, g, rows):
+            nc.tensor.matmul_mx(
+                out=out,
+                lhsT=b_words[:, c, g, t].bitcast(FP8X4),
+                lhsT_scale=b_planes[4 * g : P, c, t],
+                rhs=h0_words[:, g, rows].bitcast(FP8X4),
+                rhs_scale=h0_scales[:, g, rows],
+                start=(g == 0),
+                stop=(g == PASSES - 1),
+            )
+
+        def scale_by_s2(acc, h2, c, t, rows):
+            nc.scalar.activation(out=h2[:, t, rows], in_=acc, func=COPY, scale=s2_by_k[:, c, t : t + 1])
+
+        def interleave_h2(copy, h2, h2_by_k, rows):
+            copy(out=h2_by_k[:, rows], in_=h2[:, :, rows].rearrange("p t r -> p r t"))
+
+        def quantise_h2(h2_by_k, c, rows):
             nc.vector.quantize_mx(
                 out=h2_words[:, c, rows].bitcast(FP8X4),
                 scales=h2_scales[:, c, rows],
-                in_=h2_by_k[:].rearrange("p j r t -> p (j r t)"),
+                in_=h2_by_k[:, rows].rearrange("p r t -> p (r t)"),
             )
+
+        def finish_h2(h2, c):
+            h2_by_k = work.tile([P, TOKENS, PACK], BF16, align_bytes=64)
+            for rows in HALVES:
+                interleave_h2(nc.vector.tensor_copy, h2, h2_by_k, rows)
+            for rows in HALVES:
+                quantise_h2(h2_by_k, c, rows)
 
         results = []
 
-        def second_product(i, first_col, width):
+        def second_pass(acc, i, c, local, g):
             rows = slice(i * P, (i + 1) * P)
-            cols = slice(first_col, first_col + width)
+            nc.tensor.matmul_mx(
+                out=acc[:, 0 : local.stop - local.start],
+                lhsT=h2_words[:, g, rows].bitcast(FP8X4),
+                lhsT_scale=h2_scales[:, g, rows],
+                rhs=a_words[:, c, g, local].bitcast(FP8X4),
+                rhs_scale=a_planes[4 * g : P, c * N_TILE + local.start : c * N_TILE + local.stop],
+                start=(g == 0),
+                stop=(g == PASSES - 1),
+            )
+
+        def second_product(i, c, local):
             acc = psum.tile([P, N_TILE], F32, tag="acc", bufs=5)
             for g in range(PASSES):
-                mx_pass(nc, acc[:, 0:width], h2_words, h2_scales, rows, a_words, a_planes, cols, g)
+                second_pass(acc, i, c, local, g)
+            take_out(acc, i, c, local)
+
+        def take_out(acc, i, c, local):
+            rows = slice(i * P, (i + 1) * P)
+            cols = slice(c * N_TILE + local.start, c * N_TILE + local.stop)
+            width = local.stop - local.start
             result = work.tile([P, N_TILE], F32, bufs=6)
             nc.vector.tensor_tensor(out=result[:, 0:width], in0=acc[:, 0:width], in1=s4_all[:, cols], op=MULT)
             if results:
@@ -211,62 +225,87 @@ def tile_doublebinarylinear_kernel(
             nc.vector.tensor_tensor(out=done, in0=done, in1=bias_all[:, cols], op=ADD)
             nc.sync.dma_start(out=out_rows[rows, cols], in_=done)
 
-        def spread_s2(c):
-            cols = slice(c * N_TILE, (c + 1) * N_TILE)
-            acc = psum.tile([P, N_TILE], F32, tag="acc", bufs=5)
-            nc.tensor.matmul(acc[:], lhsT=ones[:], rhs=s2_row[:, cols], start=True, stop=True)
-            nc.scalar.copy(out=s2_all[:, cols], in_=acc[:])
-
-        def turn_s0():
-            s0_t = psum.tile([P, PACK, P], BF16, tag="transposed", bufs=3)
+        def turn_scalings():
+            s_t = psum.tile([P, PACK, P], BF16, tag="transposed", bufs=3)
             for t in range(PACK):
-                nc.tensor.transpose(s0_t[:, t, :], s0_rows[:, t:K_PASS:PACK], ident_bf16[:])
-            nc.scalar.copy(out=s0_by_k[:], in_=s0_t[:, :, 0:PASSES].rearrange("p t g -> p g t"))
+                nc.tensor.transpose(s_t[:, t, :], s_rows[:, t:K_PASS:PACK], ident_bf16[:])
+            nc.scalar.copy(out=s0_by_k[:], in_=s_t[:, :, 0:PASSES].rearrange("p t g -> p g t"))
+            nc.scalar.copy(out=s2_by_k[:], in_=s_t[:, :, PASSES : PASSES + CHUNKS].rearrange("p t c -> p c t"))
 
         def warm_up(count):
             acc = psum.tile([P, N_TILE], F32, tag="acc", bufs=5)
             for n in range(count):
                 nc.tensor.matmul(acc[:], lhsT=ones[:], rhs=warm[:], start=True, stop=True)
 
+        def open_accs():
+            accs = []
+            for n in range(PACK):
+                acc = psum.tile([P, N_TILE], F32, tag="acc", bufs=5)
+                accs.append(acc)
+            return accs
+
+        every = slice(0, TOKENS)
+        whole = slice(0, N_TILE)
         warm_up(6)
-        turn_s0()
+        turn_scalings()
+        order_b_planes(0)
         quantise_x(0)
-        for c in range(CHUNKS):
-            spread_s2(c)
+        order_b_words(0, slice(0, 1))
         quantise_x(1)
-        accs = []
-        for i in range(TOKEN_TILES):
-            acc = psum.tile([P, N_TILE], F32, tag="acc", bufs=5)
-            accs.append(acc)
+        order_b_words(0, slice(1, 2))
+        accs = open_accs()
+        h2 = work.tile([P, PACK, TOKENS], BF16)
         for g in range(PASSES):
-            for i in range(TOKEN_TILES):
-                first_pass(accs[i], i, 0, g)
+            for t in range(PACK):
+                first_pass(accs[t][:], 0, t, g, every)
                 if g == PASSES - 1:
-                    scale_by_s2(accs[i], i, 0)
+                    scale_by_s2(accs[t][:], h2, 0, t, every)
             if g + 2 < PASSES:
                 quantise_x(g + 2)
+                order_b_words(0, slice(g + 2, g + 3))
+        order_b_planes(1)
+        order_b_words(1, slice(0, PASSES))
         for c in range(1, CHUNKS - 1):
-            first_product(0, c)
-            first_product(1, c)
-            quantise_h2(0, c - 1)
-            quantise_h2(1, c - 1)
-            first_product(2, c)
-            first_product(3, c)
-        for i in range(TOKEN_TILES - 1):
-            first_product(i, CHUNKS - 1)
-        quantise_h2(0, CHUNKS - 2)
-        quantise_h2(1, CHUNKS - 2)
-        quantise_h2(0, CHUNKS - 1)
-        first_product(TOKEN_TILES - 1, CHUNKS - 1)
-        for c in range(CHUNKS):
+            order_b_planes(c + 1)
+            order_b_words(c + 1, slice(0, PASSES))
+            finish_h2(h2, c - 1)
+            h2 = work.tile([P, PACK, TOKENS], BF16)
+            for t in range(PACK):
+                acc = psum.tile([P, N_TILE], F32, tag="acc", bufs=5)
+                for g in range(PASSES):
+                    first_pass(acc[:], c, t, g, every)
+                scale_by_s2(acc[:], h2, c, t, every)
+        c = CHUNKS - 1
+        finish_h2(h2, c - 1)
+        h2 = work.tile([P, PACK, TOKENS], BF16)
+        h2_by_k = work.tile([P, TOKENS, PACK], BF16, align_bytes=64)
+        for rows in HALVES:
+            for t0 in range(0, PACK, 2):
+                acc = psum.tile([P, N_TILE], F32, tag="acc", bufs=5)
+                parts = [acc[:, 0:PAIR], acc[:, PAIR : 2 * PAIR]]
+                for j in range(2):
+                    for g in range(PASSES):
+                        first_pass(parts[j], c, t0 + j, g, rows)
+                for j in range(2):
+                    scale_by_s2(parts[j], h2, c, t0 + j, rows)
+        interleave_h2(nc.vector.tensor_copy, h2, h2_by_k, HALVES[0])
+        interleave_h2(nc.scalar.copy, h2, h2_by_k, HALVES[1])
+        quantise_h2(h2_by_k, c, HALVES[0])
+        second_product(0, 0, whole)
+        second_product(1, 0, whole)
+        second_product(0, 1, whole)
+        quantise_h2(h2_by_k, c, HALVES[1])
+        second_product(1, 1, whole)
+        for c in range(2):
+            for i in (2, 3):
+                second_product(i, c, whole)
+        for c in range(2, CHUNKS):
             for i in range(TOKEN_TILES):
                 if (i, c) == (TOKEN_TILES - 1, CHUNKS - 1):
-                    for first_col in (c * N_TILE, c * N_TILE + N_TILE // 2):
-                        second_product(i, first_col, N_TILE // 2)
+                    for first in (0, N_TILE // 2):
+                        second_product(i, c, slice(first, first + N_TILE // 2))
                 else:
-                    second_product(i, c * N_TILE, N_TILE)
-                if (i, c) == (0, 0):
-                    quantise_h2(1, CHUNKS - 1)
+                    second_product(i, c, whole)
                 if (i, c) == (1, CHUNKS - 1):
                     finish_result()
         finish_result()

@@ -64,7 +64,7 @@ def tile_doublebinarylinear_kernel(
         bias_all = keep.tile([P, DIM], BF16)
         b_loaded = keep.tile([P, CHUNKS, PASSES, N_TILE], U32, align_bytes=64)
         b_planes_loaded = keep.tile([P, DIM], U8, align_bytes=64)
-        b_words = keep.tile([P, CHUNKS, PASSES, PACK, LANES], U32, align_bytes=64)
+        b_words = keep.tile([P, CHUNKS, PACK, PASSES, LANES], U32, align_bytes=64)
         b_planes = keep.tile([P, CHUNKS, PACK, LANES], U8, align_bytes=64)
         a_words = keep.tile([P, CHUNKS, PASSES, N_TILE], U32, align_bytes=64)
         a_planes = keep.tile([P, DIM], U8, align_bytes=64)
@@ -148,20 +148,21 @@ def tile_doublebinarylinear_kernel(
 
         def order_b_words(c, passes):
             nc.vector.tensor_copy(
-                out=b_words[:, c, passes].bitcast(I32),
-                in_=b_loaded[:, c, passes].bitcast(I32).rearrange("p g (m t) -> p g t m", t=PACK),
+                out=b_words[:, c, :, passes].bitcast(I32).rearrange("p t g (r i) -> p (g r) t i", i=4),
+                in_=b_loaded[:, c, passes].bitcast(I32).rearrange("p g (r i t) -> p (g r) t i", i=4, t=PACK),
             )
 
         def order_b_planes(c):
             cols = slice(c * N_TILE, (c + 1) * N_TILE)
             nc.vector.tensor_copy(
-                out=b_planes[:, c], in_=b_planes_loaded[:, cols].rearrange("p (m t) -> p t m", t=PACK)
+                out=b_planes[:, c].rearrange("p t (r i) -> p r t i", i=16),
+                in_=b_planes_loaded[:, cols].rearrange("p (r i t) -> p r t i", i=16, t=PACK),
             )
 
         def first_pass(out, c, t, g, rows):
             nc.tensor.matmul_mx(
                 out=out,
-                lhsT=b_words[:, c, g, t].bitcast(FP8X4),
+                lhsT=b_words[:, c, t, g].bitcast(FP8X4),
                 lhsT_scale=b_planes[4 * g : P, c, t],
                 rhs=h0_words[:, g, rows].bitcast(FP8X4),
                 rhs_scale=h0_scales[:, g, rows],
@@ -173,7 +174,10 @@ def tile_doublebinarylinear_kernel(
             nc.scalar.activation(out=h2[:, t, rows], in_=acc, func=COPY, scale=s2_by_k[:, c, t : t + 1])
 
         def interleave_h2(copy, h2, h2_by_k, rows):
-            copy(out=h2_by_k[:, rows], in_=h2[:, :, rows].rearrange("p t r -> p r t"))
+            copy(
+                out=h2_by_k[:, rows].rearrange("p (r i) t -> p r t i", i=4),
+                in_=h2[:, :, rows].rearrange("p t (r i) -> p r t i", i=4),
+            )
 
         def quantise_h2(h2_by_k, c, rows):
             nc.vector.quantize_mx(

@@ -23,6 +23,7 @@ CHUNKS = DIM // N_TILE
 LANES = N_TILE // PACK
 QUADRANTS = 4
 WORDS_PER_PASS = K_PASS // 2
+LAID_OUT_PASSES = (2, 3)
 TOKEN_PAIRS = TOKEN_TILES // 2
 PAIR = 2 * P
 HALVES = (slice(0, PAIR), slice(PAIR, TOKENS))
@@ -57,7 +58,8 @@ def tile_doublebinarylinear_kernel(
         name="psum", bufs=1
     ) as psum, tc.manual_schedule():
         x_sb = keep.tile([P, PASSES, TOKEN_TILES, K_PASS], BF16)
-        s_rows = keep.tile([P, K_PASS], BF16)
+        s0_rows = keep.tile([P, K_PASS], BF16)
+        s2_rows = keep.tile([P, K_PASS], BF16)
         s0_by_k = keep.tile([P, PASSES, PACK], BF16)
         s2_by_k = keep.tile([P, CHUNKS, PACK], F32)
         s4_all = keep.tile([P, DIM], BF16)
@@ -74,13 +76,12 @@ def tile_doublebinarylinear_kernel(
         h2_scales = keep.tile([P, PASSES, TOKENS], U8, align_bytes=64)
         ident_f32 = keep.tile([P, P], F32)
         ident_bf16 = keep.tile([P, P], BF16)
-        ones = keep.tile([P, P], BF16)
         warm = keep.tile([P, N_TILE], BF16)
 
-        nc.vector.memset(ones[:], 1.0)
         nc.vector.memset(warm[:].bitcast(I32), 0)
-        nc.vector.memset(s_rows[:].bitcast(I32), 0)
+        nc.vector.memset(s0_rows[:].bitcast(I32), 0)
         nc.vector.memset(b_planes_loaded[:].bitcast(I32), 0)
+        nc.vector.memset(s2_rows[:].bitcast(I32), 0)
         nc.vector.memset(a_planes[:].bitcast(I32), 0)
         make_identity(nc, ident_bf16[:])
         make_identity(nc, ident_f32[:])
@@ -100,10 +101,7 @@ def tile_doublebinarylinear_kernel(
 
         load_x(0, slice(0, 2))
         load_x(0, slice(2, 4))
-        nc.sync.dma_start(out=s_rows[0:PASSES, :], in_=scaling0.rearrange("(g k) -> g k", g=PASSES))
-        nc.sync.dma_start(
-            out=s_rows[PASSES : PASSES + CHUNKS, :], in_=scaling2.rearrange("(c k) -> c k", c=CHUNKS)
-        )
+        nc.sync.dma_start(out=s0_rows[0:PASSES, :], in_=scaling0.rearrange("(g k) -> g k", g=PASSES))
         load_scale_planes(nc, b_planes_loaded, B_scales, slice(0, N_TILE))
         load_word_pass(0)
         load_x(1, slice(0, 4))
@@ -111,6 +109,7 @@ def tile_doublebinarylinear_kernel(
         for g in range(2, PASSES):
             load_x(g, slice(0, 4))
             load_word_pass(g)
+        nc.sync.dma_start(out=s2_rows[0:CHUNKS, :], in_=scaling2.rearrange("(c k) -> c k", c=CHUNKS))
         load_scale_planes(nc, b_planes_loaded, B_scales, slice(N_TILE, DIM))
         for c in range(1, CHUNKS):
             load_word_chunk(nc, b_loaded, B_words, c)
@@ -127,10 +126,16 @@ def tile_doublebinarylinear_kernel(
             for pair in range(TOKEN_PAIRS):
                 rows = slice(pair * PAIR, (pair + 1) * PAIR)
                 pairs_t = psum.tile([P, 2, 2, P], F32, tag="transposed", bufs=3)
+                if g in LAID_OUT_PASSES:
+                    x_split = work.tile([P, 2, 2, P], F32)
+                    for j in range(2):
+                        x_words = x_sb[:, g, 2 * pair + j, :].bitcast(F32)
+                        nc.scalar.copy(out=x_split[:, j], in_=x_words.rearrange("r (p u) -> r u p", u=2))
                 for j in range(2):
                     x_words = x_sb[:, g, 2 * pair + j, :].bitcast(F32)
                     for u in range(2):
-                        nc.tensor.transpose(pairs_t[:, u, j, :], x_words[:, u:WORDS_PER_PASS:2], ident_f32[:])
+                        words = x_split[:, j, u, :] if g in LAID_OUT_PASSES else x_words[:, u:WORDS_PER_PASS:2]
+                        nc.tensor.transpose(pairs_t[:, u, j, :], words, ident_f32[:])
                 x_t = pairs_t[:].rearrange("p u j r -> p (u j r)").bitcast(BF16)
                 nc.vector.tensor_tensor(
                     out=h0[:, rows].rearrange("p r (u e) -> p r u e", u=2),
@@ -138,13 +143,10 @@ def tile_doublebinarylinear_kernel(
                     in1=s0_by_k[:, g].rearrange("p (u e) -> p u e", u=2).unsqueeze(1).to_broadcast([P, PAIR, 2, 2]),
                     op=MULT,
                 )
-            for pair in range(TOKEN_PAIRS):
-                rows = slice(pair * PAIR, (pair + 1) * PAIR)
-                nc.vector.quantize_mx(
-                    out=h0_words[:, g, rows].bitcast(FP8X4),
-                    scales=h0_scales[:, g, rows],
-                    in_=h0[:, rows].rearrange("p r t -> p (r t)"),
-                )
+            order_b_words(0, slice(g, g + 1))
+            nc.vector.quantize_mx(
+                out=h0_words[:, g].bitcast(FP8X4), scales=h0_scales[:, g], in_=h0[:].rearrange("p r t -> p (r t)")
+            )
 
         def order_b_words(c, passes):
             nc.vector.tensor_copy(
@@ -186,12 +188,11 @@ def tile_doublebinarylinear_kernel(
                 in_=h2_by_k[:, rows].rearrange("p r t -> p (r t)"),
             )
 
-        def finish_h2(h2, c):
+        def interleave_halves(h2):
             h2_by_k = work.tile([P, TOKENS, PACK], BF16, align_bytes=64)
-            for rows in HALVES:
-                interleave_h2(nc.vector.tensor_copy, h2, h2_by_k, rows)
-            for rows in HALVES:
-                quantise_h2(h2_by_k, c, rows)
+            interleave_h2(nc.vector.tensor_copy, h2, h2_by_k, HALVES[0])
+            interleave_h2(nc.scalar.copy, h2, h2_by_k, HALVES[1])
+            return h2_by_k
 
         results = []
 
@@ -229,17 +230,16 @@ def tile_doublebinarylinear_kernel(
             nc.vector.tensor_tensor(out=done, in0=done, in1=bias_all[:, cols], op=ADD)
             nc.sync.dma_start(out=out_rows[rows, cols], in_=done)
 
-        def turn_scalings():
+        def turn_scaling(s_rows, s_by_k):
             s_t = psum.tile([P, PACK, P], BF16, tag="transposed", bufs=3)
             for t in range(PACK):
                 nc.tensor.transpose(s_t[:, t, :], s_rows[:, t:K_PASS:PACK], ident_bf16[:])
-            nc.scalar.copy(out=s0_by_k[:], in_=s_t[:, :, 0:PASSES].rearrange("p t g -> p g t"))
-            nc.scalar.copy(out=s2_by_k[:], in_=s_t[:, :, PASSES : PASSES + CHUNKS].rearrange("p t c -> p c t"))
+            nc.scalar.copy(out=s_by_k[:], in_=s_t[:, :, 0:PASSES].rearrange("p t g -> p g t"))
 
         def warm_up(count):
             acc = psum.tile([P, N_TILE], F32, tag="acc", bufs=5)
             for n in range(count):
-                nc.tensor.matmul(acc[:], lhsT=ones[:], rhs=warm[:], start=True, stop=True)
+                nc.tensor.matmul(acc[:], lhsT=warm[:, 0:P], rhs=warm[:], start=True, stop=True)
 
         def open_accs():
             accs = []
@@ -250,13 +250,12 @@ def tile_doublebinarylinear_kernel(
 
         every = slice(0, TOKENS)
         whole = slice(0, N_TILE)
-        warm_up(6)
-        turn_scalings()
+        warm_up(3)
+        turn_scaling(s0_rows, s0_by_k)
         order_b_planes(0)
         quantise_x(0)
-        order_b_words(0, slice(0, 1))
+        warm_up(2)
         quantise_x(1)
-        order_b_words(0, slice(1, 2))
         accs = open_accs()
         h2 = work.tile([P, PACK, TOKENS], BF16)
         for g in range(PASSES):
@@ -266,13 +265,16 @@ def tile_doublebinarylinear_kernel(
                     scale_by_s2(accs[t][:], h2, 0, t, every)
             if g + 2 < PASSES:
                 quantise_x(g + 2)
-                order_b_words(0, slice(g + 2, g + 3))
+            if g == 1:
+                turn_scaling(s2_rows, s2_by_k)
         order_b_planes(1)
         order_b_words(1, slice(0, PASSES))
         for c in range(1, CHUNKS - 1):
+            h2_by_k = interleave_halves(h2)
             order_b_planes(c + 1)
             order_b_words(c + 1, slice(0, PASSES))
-            finish_h2(h2, c - 1)
+            for rows in HALVES:
+                quantise_h2(h2_by_k, c - 1, rows)
             h2 = work.tile([P, PACK, TOKENS], BF16)
             for t in range(PACK):
                 acc = psum.tile([P, N_TILE], F32, tag="acc", bufs=5)
@@ -280,9 +282,10 @@ def tile_doublebinarylinear_kernel(
                     first_pass(acc[:], c, t, g, every)
                 scale_by_s2(acc[:], h2, c, t, every)
         c = CHUNKS - 1
-        finish_h2(h2, c - 1)
+        h2_by_k = interleave_halves(h2)
+        for rows in HALVES:
+            quantise_h2(h2_by_k, c - 1, rows)
         h2 = work.tile([P, PACK, TOKENS], BF16)
-        h2_by_k = work.tile([P, TOKENS, PACK], BF16, align_bytes=64)
         for rows in HALVES:
             for t0 in range(0, PACK, 2):
                 acc = psum.tile([P, N_TILE], F32, tag="acc", bufs=5)
@@ -292,8 +295,7 @@ def tile_doublebinarylinear_kernel(
                         first_pass(parts[j], c, t0 + j, g, rows)
                 for j in range(2):
                     scale_by_s2(parts[j], h2, c, t0 + j, rows)
-        interleave_h2(nc.vector.tensor_copy, h2, h2_by_k, HALVES[0])
-        interleave_h2(nc.scalar.copy, h2, h2_by_k, HALVES[1])
+        h2_by_k = interleave_halves(h2)
         quantise_h2(h2_by_k, c, HALVES[0])
         second_product(0, 0, whole)
         second_product(1, 0, whole)

@@ -66,14 +66,20 @@ def tile_doublebinarylinear_kernel(
         bias_all = keep.tile([P, DIM], BF16)
         b_loaded = keep.tile([P, CHUNKS, PASSES, N_TILE], U32, align_bytes=64)
         b_planes_loaded = keep.tile([P, DIM], U8, align_bytes=64)
-        b_words = keep.tile([P, CHUNKS, PACK, PASSES, LANES], U32, align_bytes=64)
-        b_planes = keep.tile([P, CHUNKS, PACK, LANES], U8, align_bytes=64)
-        a_words = keep.tile([P, CHUNKS, PASSES, N_TILE], U32, align_bytes=64)
-        a_planes = keep.tile([P, DIM], U8, align_bytes=64)
-        h0_words = keep.tile([P, PASSES, TOKENS], U32, align_bytes=64)
-        h0_scales = keep.tile([P, PASSES, TOKENS], U8, align_bytes=64)
-        h2_words = keep.tile([P, PASSES, TOKENS], U32, align_bytes=64)
-        h2_scales = keep.tile([P, PASSES, TOKENS], U8, align_bytes=64)
+        b_words_at_64 = keep.tile([P, 16 + CHUNKS * PACK * PASSES * LANES], U32, align_bytes=256)
+        b_words = b_words_at_64[:, 16:].rearrange("p (c g t m) -> p c g t m", c=CHUNKS, g=PASSES, t=PACK)
+        b_planes_at_192 = keep.tile([P, 192 + CHUNKS * PACK * LANES], U8, align_bytes=256)
+        b_planes = b_planes_at_192[:, 192:].rearrange("p (c t m) -> p c t m", c=CHUNKS, t=PACK)
+        a_words = keep.tile([P, CHUNKS, PASSES, N_TILE], U32, align_bytes=256)
+        a_planes_at_128 = keep.tile([P, 128 + DIM], U8, align_bytes=256)
+        a_planes = a_planes_at_128[:, 128:]
+        h0_words = keep.tile([P, PASSES, TOKENS], U32, align_bytes=256)
+        h0_scales_at_128 = keep.tile([P, 128 + PASSES * TOKENS], U8, align_bytes=256)
+        h0_scales = h0_scales_at_128[:, 128:].rearrange("p (g r) -> p g r", g=PASSES)
+        h2_words_at_64 = keep.tile([P, 16 + PASSES * TOKENS], U32, align_bytes=256)
+        h2_words = h2_words_at_64[:, 16:].rearrange("p (g r) -> p g r", g=PASSES)
+        h2_scales_at_192 = keep.tile([P, 192 + PASSES * TOKENS], U8, align_bytes=256)
+        h2_scales = h2_scales_at_192[:, 192:].rearrange("p (g r) -> p g r", g=PASSES)
         ident_f32 = keep.tile([P, P], F32)
         ident_bf16 = keep.tile([P, P], BF16)
         warm = keep.tile([P, N_TILE], BF16)
@@ -82,7 +88,7 @@ def tile_doublebinarylinear_kernel(
         nc.vector.memset(s0_rows[:].bitcast(I32), 0)
         nc.vector.memset(b_planes_loaded[:].bitcast(I32), 0)
         nc.vector.memset(s2_rows[:].bitcast(I32), 0)
-        nc.vector.memset(a_planes[:].bitcast(I32), 0)
+        nc.vector.memset(a_planes.bitcast(I32), 0)
         make_identity(nc, ident_bf16[:])
         make_identity(nc, ident_f32[:])
 
@@ -105,11 +111,11 @@ def tile_doublebinarylinear_kernel(
         load_scale_planes(nc, b_planes_loaded, B_scales, slice(0, N_TILE))
         load_word_pass(0)
         load_x(1, slice(0, 4))
+        nc.sync.dma_start(out=s2_rows[0:CHUNKS, :], in_=scaling2.rearrange("(c k) -> c k", c=CHUNKS))
         load_word_pass(1)
         for g in range(2, PASSES):
             load_x(g, slice(0, 4))
             load_word_pass(g)
-        nc.sync.dma_start(out=s2_rows[0:CHUNKS, :], in_=scaling2.rearrange("(c k) -> c k", c=CHUNKS))
         load_scale_planes(nc, b_planes_loaded, B_scales, slice(N_TILE, DIM))
         for c in range(1, CHUNKS):
             load_word_chunk(nc, b_loaded, B_words, c)
@@ -150,13 +156,13 @@ def tile_doublebinarylinear_kernel(
 
         def order_b_words(c, passes):
             nc.vector.tensor_copy(
-                out=b_words[:, c, :, passes].bitcast(I32).rearrange("p t g (r i) -> p (g r) t i", i=4),
-                in_=b_loaded[:, c, passes].bitcast(I32).rearrange("p g (r i t) -> p (g r) t i", i=4, t=PACK),
+                out=b_words[:, c, passes].bitcast(I32).rearrange("p g t (r i) -> p g r t i", i=4),
+                in_=b_loaded[:, c, passes].bitcast(I32).rearrange("p g (r i t) -> p g r t i", i=4, t=PACK),
             )
 
-        def order_b_planes(c):
+        def order_b_planes(engine, c):
             cols = slice(c * N_TILE, (c + 1) * N_TILE)
-            nc.vector.tensor_copy(
+            engine.tensor_copy(
                 out=b_planes[:, c].rearrange("p t (r i) -> p r t i", i=16),
                 in_=b_planes_loaded[:, cols].rearrange("p (r i t) -> p r t i", i=16, t=PACK),
             )
@@ -164,7 +170,7 @@ def tile_doublebinarylinear_kernel(
         def first_pass(out, c, t, g, rows):
             nc.tensor.matmul_mx(
                 out=out,
-                lhsT=b_words[:, c, t, g].bitcast(FP8X4),
+                lhsT=b_words[:, c, g, t].bitcast(FP8X4),
                 lhsT_scale=b_planes[4 * g : P, c, t],
                 rhs=h0_words[:, g, rows].bitcast(FP8X4),
                 rhs_scale=h0_scales[:, g, rows],
@@ -252,10 +258,11 @@ def tile_doublebinarylinear_kernel(
         whole = slice(0, N_TILE)
         warm_up(3)
         turn_scaling(s0_rows, s0_by_k)
-        order_b_planes(0)
+        order_b_planes(nc.gpsimd, 0)
         quantise_x(0)
         warm_up(2)
         quantise_x(1)
+        turn_scaling(s2_rows, s2_by_k)
         accs = open_accs()
         h2 = work.tile([P, PACK, TOKENS], BF16)
         for g in range(PASSES):
@@ -265,13 +272,12 @@ def tile_doublebinarylinear_kernel(
                     scale_by_s2(accs[t][:], h2, 0, t, every)
             if g + 2 < PASSES:
                 quantise_x(g + 2)
-            if g == 1:
-                turn_scaling(s2_rows, s2_by_k)
-        order_b_planes(1)
-        order_b_words(1, slice(0, PASSES))
+        order_b_planes(nc.vector, 1)
+        for g in range(PASSES):
+            order_b_words(1, slice(g, g + 1))
         for c in range(1, CHUNKS - 1):
             h2_by_k = interleave_halves(h2)
-            order_b_planes(c + 1)
+            order_b_planes(nc.vector, c + 1)
             order_b_words(c + 1, slice(0, PASSES))
             for rows in HALVES:
                 quantise_h2(h2_by_k, c - 1, rows)

import concourse.mybir as mybir
from concourse.masks import make_identity

F32 = mybir.dt.float32
BF16 = mybir.dt.bfloat16
I32 = mybir.dt.int32
U32 = mybir.dt.uint32
U8 = mybir.dt.uint8
FP8X4 = mybir.dt.float8_e4m3fn_x4
MULT = mybir.AluOpType.mult
ADD = mybir.AluOpType.add
COPY = mybir.ActivationFunctionType.Copy

P = 128
PACK = 4
K_PASS = P * PACK
TOKENS = 512
DIM = 2048
TOKEN_TILES = TOKENS // P
PASSES = DIM // K_PASS
N_TILE = 512
CHUNKS = DIM // N_TILE
LANES = N_TILE // PACK
QUADRANTS = 4
WORDS_PER_PASS = K_PASS // 2
LAID_OUT_PASSES = (2, 3)
TOKEN_PAIRS = TOKEN_TILES // 2
PAIR = 2 * P
HALVES = (slice(0, PAIR), slice(PAIR, TOKENS))

FLOPS = 2 * 2 * TOKENS * DIM * DIM


def load_scale_planes(nc, planes, scales, cols):
    for quadrant in range(QUADRANTS):
        nc.sync.dma_start(
            out=planes[32 * quadrant : 32 * quadrant + 4 * PASSES, cols].bitcast(I32),
            in_=scales[:, 4 * quadrant : 4 * quadrant + 4, cols].bitcast(I32),
        )


def load_word_chunk(nc, words, words_dram, chunk):
    byte_cols = slice(chunk * N_TILE * PACK, (chunk + 1) * N_TILE * PACK)
    nc.sync.dma_start(
        out=words[:, chunk].bitcast(I32),
        in_=words_dram.rearrange("g p n t -> p g (n t)")[:, :, byte_cols].bitcast(I32),
    )


def tile_doublebinarylinear_kernel(
    tc, x, scaling0, B_words, B_scales, scaling2, A_words, A_scales, scaling4, bias, out
):
    nc = tc.nc
    x_rows = x.flatten_outer_dims()
    out_rows = out.flatten_outer_dims()

    with tc.tile_pool(name="keep", bufs=1) as keep, tc.tile_pool(name="work", bufs=2) as work, tc.psum_pool(
        name="psum", bufs=1
    ) as psum, tc.manual_schedule():
        x_sb = keep.tile([P, PASSES, TOKEN_TILES, K_PASS], BF16)
        s0_rows = keep.tile([P, K_PASS], BF16)
        s2_rows = keep.tile([P, K_PASS], BF16)
        s0_by_k = keep.tile([P, PASSES, PACK], BF16)
        s2_by_k = keep.tile([P, CHUNKS, PACK], F32)
        s4_all = keep.tile([P, DIM], BF16)
        bias_all = keep.tile([P, DIM], BF16)
        b_loaded = keep.tile([P, CHUNKS, PASSES, N_TILE], U32, align_bytes=64)
        b_planes_loaded = keep.tile([P, DIM], U8, align_bytes=64)
        b_words_at_64 = keep.tile([P, 16 + CHUNKS * PACK * PASSES * LANES], U32, align_bytes=256)
        b_words = b_words_at_64[:, 16:].rearrange("p (c g t m) -> p c g t m", c=CHUNKS, g=PASSES, t=PACK)
        b_planes_at_192 = keep.tile([P, 192 + CHUNKS * PACK * LANES], U8, align_bytes=256)
        b_planes = b_planes_at_192[:, 192:].rearrange("p (c t m) -> p c t m", c=CHUNKS, t=PACK)
        a_words = keep.tile([P, CHUNKS, PASSES, N_TILE], U32, align_bytes=256)
        a_planes_at_128 = keep.tile([P, 128 + DIM], U8, align_bytes=256)
        a_planes = a_planes_at_128[:, 128:]
        h0_words = keep.tile([P, PASSES, TOKENS], U32, align_bytes=256)
        h0_scales_at_128 = keep.tile([P, 128 + PASSES * TOKENS], U8, align_bytes=256)
        h0_scales = h0_scales_at_128[:, 128:].rearrange("p (g r) -> p g r", g=PASSES)
        h2_words_at_64 = keep.tile([P, 16 + PASSES * TOKENS], U32, align_bytes=256)
        h2_words = h2_words_at_64[:, 16:].rearrange("p (g r) -> p g r", g=PASSES)
        h2_scales_at_192 = keep.tile([P, 192 + PASSES * TOKENS], U8, align_bytes=256)
        h2_scales = h2_scales_at_192[:, 192:].rearrange("p (g r) -> p g r", g=PASSES)
        ident_f32 = keep.tile([P, P], F32)
        ident_bf16 = keep.tile([P, P], BF16)
        warm = keep.tile([P, N_TILE], BF16)

        nc.vector.memset(warm[:].bitcast(I32), 0)
        nc.vector.memset(s0_rows[:].bitcast(I32), 0)
        nc.vector.memset(b_planes_loaded[:].bitcast(I32), 0)
        nc.vector.memset(s2_rows[:].bitcast(I32), 0)
        nc.vector.memset(a_planes.bitcast(I32), 0)
        make_identity(nc, ident_bf16[:])
        make_identity(nc, ident_f32[:])

        x_by_tile = x_rows.rearrange("(i p) k -> p i k", p=P)

        def load_x(g, tiles):
            ks = slice(g * K_PASS, (g + 1) * K_PASS)
            nc.sync.dma_start(out=x_sb[:, g, tiles, :], in_=x_by_tile[:, tiles, ks])

        def load_word_pass(g):
            byte_cols = slice(0, N_TILE * PACK)
            nc.sync.dma_start(
                out=b_loaded[:, 0, g].bitcast(I32),
                in_=B_words[g].rearrange("p n t -> p (n t)")[:, byte_cols].bitcast(I32),
            )

        load_x(0, slice(0, 2))
        load_x(0, slice(2, 4))
        nc.sync.dma_start(out=s0_rows[0:PASSES, :], in_=scaling0.rearrange("(g k) -> g k", g=PASSES))
        load_scale_planes(nc, b_planes_loaded, B_scales, slice(0, N_TILE))
        load_word_pass(0)
        load_x(1, slice(0, 4))
        nc.sync.dma_start(out=s2_rows[0:CHUNKS, :], in_=scaling2.rearrange("(c k) -> c k", c=CHUNKS))
        load_word_pass(1)
        for g in range(2, PASSES):
            load_x(g, slice(0, 4))
            load_word_pass(g)
        load_scale_planes(nc, b_planes_loaded, B_scales, slice(N_TILE, DIM))
        for c in range(1, CHUNKS):
            load_word_chunk(nc, b_loaded, B_words, c)
        load_scale_planes(nc, a_planes, A_scales, slice(0, DIM))
        for c in range(2):
            load_word_chunk(nc, a_words, A_words, c)
        nc.sync.dma_start(out=s4_all[:], in_=scaling4.partition_broadcast(P))
        nc.sync.dma_start(out=bias_all[:], in_=bias.partition_broadcast(P))
        for c in range(2, CHUNKS):
            load_word_chunk(nc, a_words, A_words, c)

        def quantise_x(g):
            h0 = work.tile([P, TOKENS, PACK], BF16, align_bytes=64)
            for pair in range(TOKEN_PAIRS):
                rows = slice(pair * PAIR, (pair + 1) * PAIR)
                pairs_t = psum.tile([P, 2, 2, P], F32, tag="transposed", bufs=3)
                if g in LAID_OUT_PASSES:
                    x_split = work.tile([P, 2, 2, P], F32)
                    for j in range(2):
                        x_words = x_sb[:, g, 2 * pair + j, :].bitcast(F32)
                        nc.scalar.copy(out=x_split[:, j], in_=x_words.rearrange("r (p u) -> r u p", u=2))
                for j in range(2):
                    x_words = x_sb[:, g, 2 * pair + j, :].bitcast(F32)
                    for u in range(2):
                        words = x_split[:, j, u, :] if g in LAID_OUT_PASSES else x_words[:, u:WORDS_PER_PASS:2]
                        nc.tensor.transpose(pairs_t[:, u, j, :], words, ident_f32[:])
                x_t = pairs_t[:].rearrange("p u j r -> p (u j r)").bitcast(BF16)
                nc.vector.tensor_tensor(
                    out=h0[:, rows].rearrange("p r (u e) -> p r u e", u=2),
                    in0=x_t.rearrange("p (u r e) -> p r u e", u=2, e=2),
                    in1=s0_by_k[:, g].rearrange("p (u e) -> p u e", u=2).unsqueeze(1).to_broadcast([P, PAIR, 2, 2]),
                    op=MULT,
                )
            order_b_words(0, slice(g, g + 1))
            nc.vector.quantize_mx(
                out=h0_words[:, g].bitcast(FP8X4), scales=h0_scales[:, g], in_=h0[:].rearrange("p r t -> p (r t)")
            )

        def order_b_words(c, passes):
            nc.vector.tensor_copy(
                out=b_words[:, c, passes].bitcast(I32).rearrange("p g t (r i) -> p g r t i", i=4),
                in_=b_loaded[:, c, passes].bitcast(I32).rearrange("p g (r i t) -> p g r t i", i=4, t=PACK),
            )

        def order_b_planes(engine, c):
            cols = slice(c * N_TILE, (c + 1) * N_TILE)
            engine.tensor_copy(
                out=b_planes[:, c].rearrange("p t (r i) -> p r t i", i=16),
                in_=b_planes_loaded[:, cols].rearrange("p (r i t) -> p r t i", i=16, t=PACK),
            )

        def first_pass(out, c, t, g, rows):
            nc.tensor.matmul_mx(
                out=out,
                lhsT=b_words[:, c, g, t].bitcast(FP8X4),
                lhsT_scale=b_planes[4 * g : P, c, t],
                rhs=h0_words[:, g, rows].bitcast(FP8X4),
                rhs_scale=h0_scales[:, g, rows],
                start=(g == 0),
                stop=(g == PASSES - 1),
            )

        def scale_by_s2(acc, h2, c, t, rows):
            nc.scalar.activation(out=h2[:, t, rows], in_=acc, func=COPY, scale=s2_by_k[:, c, t : t + 1])

        def interleave_h2(copy, h2, h2_by_k, rows):
            copy(
                out=h2_by_k[:, rows].rearrange("p (r i) t -> p r t i", i=4),
                in_=h2[:, :, rows].rearrange("p t (r i) -> p r t i", i=4),
            )

        def quantise_h2(h2_by_k, c, rows):
            nc.vector.quantize_mx(
                out=h2_words[:, c, rows].bitcast(FP8X4),
                scales=h2_scales[:, c, rows],
                in_=h2_by_k[:, rows].rearrange("p r t -> p (r t)"),
            )

        def interleave_halves(h2):
            h2_by_k = work.tile([P, TOKENS, PACK], BF16, align_bytes=64)
            interleave_h2(nc.vector.tensor_copy, h2, h2_by_k, HALVES[0])
            interleave_h2(nc.scalar.copy, h2, h2_by_k, HALVES[1])
            return h2_by_k

        results = []

        def second_pass(acc, i, c, local, g):
            rows = slice(i * P, (i + 1) * P)
            nc.tensor.matmul_mx(
                out=acc[:, 0 : local.stop - local.start],
                lhsT=h2_words[:, g, rows].bitcast(FP8X4),
                lhsT_scale=h2_scales[:, g, rows],
                rhs=a_words[:, c, g, local].bitcast(FP8X4),
                rhs_scale=a_planes[4 * g : P, c * N_TILE + local.start : c * N_TILE + local.stop],
                start=(g == 0),
                stop=(g == PASSES - 1),
            )

        def second_product(i, c, local):
            acc = psum.tile([P, N_TILE], F32, tag="acc", bufs=5)
            for g in range(PASSES):
                second_pass(acc, i, c, local, g)
            take_out(acc, i, c, local)

        def take_out(acc, i, c, local):
            rows = slice(i * P, (i + 1) * P)
            cols = slice(c * N_TILE + local.start, c * N_TILE + local.stop)
            width = local.stop - local.start
            result = work.tile([P, N_TILE], F32, bufs=6)
            nc.vector.tensor_tensor(out=result[:, 0:width], in0=acc[:, 0:width], in1=s4_all[:, cols], op=MULT)
            if results:
                finish_result()
            results.append((result, rows, cols))

        def finish_result():
            result, rows, cols = results.pop(0)
            done = result[:, 0 : cols.stop - cols.start]
            nc.vector.tensor_tensor(out=done, in0=done, in1=bias_all[:, cols], op=ADD)
            nc.sync.dma_start(out=out_rows[rows, cols], in_=done)

        def turn_scaling(s_rows, s_by_k):
            s_t = psum.tile([P, PACK, P], BF16, tag="transposed", bufs=3)
            for t in range(PACK):
                nc.tensor.transpose(s_t[:, t, :], s_rows[:, t:K_PASS:PACK], ident_bf16[:])
            nc.scalar.copy(out=s_by_k[:], in_=s_t[:, :, 0:PASSES].rearrange("p t g -> p g t"))

        def warm_up(count):
            acc = psum.tile([P, N_TILE], F32, tag="acc", bufs=5)
            for n in range(count):
                nc.tensor.matmul(acc[:], lhsT=warm[:, 0:P], rhs=warm[:], start=True, stop=True)

        def open_accs():
            accs = []
            for n in range(PACK):
                acc = psum.tile([P, N_TILE], F32, tag="acc", bufs=5)
                accs.append(acc)
            return accs

        every = slice(0, TOKENS)
        whole = slice(0, N_TILE)
        warm_up(3)
        turn_scaling(s0_rows, s0_by_k)
        order_b_planes(nc.gpsimd, 0)
        quantise_x(0)
        warm_up(2)
        quantise_x(1)
        turn_scaling(s2_rows, s2_by_k)
        accs = open_accs()
        h2 = work.tile([P, PACK, TOKENS], BF16)
        for g in range(PASSES):
            for t in range(PACK):
                first_pass(accs[t][:], 0, t, g, every)
                if g == PASSES - 1:
                    scale_by_s2(accs[t][:], h2, 0, t, every)
            if g + 2 < PASSES:
                quantise_x(g + 2)
        order_b_planes(nc.vector, 1)
        for g in range(PASSES):
            order_b_words(1, slice(g, g + 1))
        for c in range(1, CHUNKS - 1):
            h2_by_k = interleave_halves(h2)
            order_b_planes(nc.vector, c + 1)
            order_b_words(c + 1, slice(0, PASSES))
            for rows in HALVES:
                quantise_h2(h2_by_k, c - 1, rows)
            h2 = work.tile([P, PACK, TOKENS], BF16)
            for t in range(PACK):
                acc = psum.tile([P, N_TILE], F32, tag="acc", bufs=5)
                for g in range(PASSES):
                    first_pass(acc[:], c, t, g, every)
                scale_by_s2(acc[:], h2, c, t, every)
        c = CHUNKS - 1
        h2_by_k = interleave_halves(h2)
        for rows in HALVES:
            quantise_h2(h2_by_k, c - 1, rows)
        h2 = work.tile([P, PACK, TOKENS], BF16)
        for rows in HALVES:
            for t0 in range(0, PACK, 2):
                acc = psum.tile([P, N_TILE], F32, tag="acc", bufs=5)
                parts = [acc[:, 0:PAIR], acc[:, PAIR : 2 * PAIR]]
                for j in range(2):
                    for g in range(PASSES):
                        first_pass(parts[j], c, t0 + j, g, rows)
                for j in range(2):
                    scale_by_s2(parts[j], h2, c, t0 + j, rows)
        h2_by_k = interleave_halves(h2)
        quantise_h2(h2_by_k, c, HALVES[0])
        second_product(0, 0, whole)
        second_product(1, 0, whole)
        second_product(0, 1, whole)
        quantise_h2(h2_by_k, c, HALVES[1])
        second_product(1, 1, whole)
        for c in range(2):
            for i in (2, 3):
                second_product(i, c, whole)
        for c in range(2, CHUNKS):
            for i in range(TOKEN_TILES):
                if (i, c) == (TOKEN_TILES - 1, CHUNKS - 1):
                    for first in (0, N_TILE // 2):
                        second_product(i, c, slice(first, first + N_TILE // 2))
                else:
                    second_product(i, c, whole)
                if (i, c) == (1, CHUNKS - 1):
                    finish_result()
        finish_result()
